import numpy as np
import ml_dtypes

BF16 = ml_dtypes.bfloat16


def bf(x):
    return np.asarray(x, np.float32).astype(BF16)


def f32(x):
    return np.asarray(x, np.float32)


def f64(x):
    return np.asarray(x).astype(np.float64)


def striped(idx):
    return np.tile(idx.reshape(-1, 16).T, (8, 1))


S, D, M, N, E1, E2 = 4096, 128, 512, 2048, 1024, 768


def setup_inputs():
    return {
        "table": bf(np.random.standard_normal((S, D))),
        "w0": bf(np.random.standard_normal((D, M)) / np.sqrt(D)),
        "b0": f32(0.1 * np.random.standard_normal((M, 1))),
        "x1": bf(np.random.standard_normal((E1, N))),
        "w1": bf(np.random.standard_normal((E1, M)) / np.sqrt(E1)),
        "b1": f32(0.1 * np.random.standard_normal((M, 1))),
        "x2": bf(np.random.standard_normal((E2, N))),
        "w2": bf(np.random.standard_normal((E2, M)) / np.sqrt(E2)),
        "b2": f32(0.1 * np.random.standard_normal((M, 1))),
        "wa": bf(np.random.standard_normal((M, 1)) / np.sqrt(M)),
        "offs": striped(np.random.permutation(S)[:N]),
    }


def reference(table, w0, b0, x1, w1, b1, x2, w2, b2, wa, offs):
    idx = offs[:16].T.reshape(-1)
    p0 = f64(w0).T @ f64(table)[idx].T + f64(b0)
    p1 = f64(w1).T @ f64(x1) + f64(b1)
    p2 = f64(w2).T @ f64(x2) + f64(b2)
    l0 = f64(wa).T @ p0
    l1 = f64(wa).T @ p1
    l2 = f64(wa).T @ p2
    t = np.maximum(np.maximum(l0, l1), l2)
    e0 = np.exp(l0 - t)
    e1 = np.exp(l1 - t)
    e2 = np.exp(l2 - t)
    return (e0 * p0 + e1 * p1 + e2 * p2) / (e0 + e1 + e2)

@@ -1,0 +1,162 @@
+from contextlib import ExitStack
+
+import concourse.mybir as mybir
+from concourse.masks import make_identity
+
+BF16, F32, U16 = mybir.dt.bfloat16, mybir.dt.float32, mybir.dt.uint16
+ACT = mybir.ActivationFunctionType
+ALU = mybir.AluOpType
+
+P = 128
+S, D, M, N, E1, E2 = 4096, 128, 512, 2048, 1024, 768
+W = 512
+PIECES = N // W
+MB = M // P
+SB = S // P
+TURNED = 8
+
+FLOPS = 2 * M * N * (D + E1 + E2) + 2 * 3 * M * N
+
+
+def tile_dynamicmetaembedding_b_kernel(tc, table, w0, b0, x1, w1, b1, x2, w2, b2, wa, offs, out):
+    nc = tc.nc
+    with ExitStack() as ctx:
+        held = ctx.enter_context(tc.tile_pool(name="held", bufs=1))
+        proj = ctx.enter_context(tc.tile_pool(name="proj", bufs=2))
+        soft = ctx.enter_context(tc.tile_pool(name="soft", bufs=2))
+        work = ctx.enter_context(tc.tile_pool(name="work", bufs=3))
+        bank = ctx.enter_context(tc.psum_pool(name="bank", bufs=7))
+        turn = ctx.enter_context(tc.psum_pool(name="turn", bufs=1))
+
+        offsets = held.tile([P, N // 16], U16, name="offsets")
+        nc.sync.dma_start(offsets[:], offs)
+
+        width = {1: E1, 2: E2}
+        x_dram = {1: x1.rearrange("(k p) j -> p k j", p=P), 2: x2.rearrange("(k p) j -> p k j", p=P)}
+        x_sb = {
+            (i, q): held.tile([P, width[i] // P, W], BF16, name="x%d_%d" % (i, q))
+            for i in (1, 2)
+            for q in range(PIECES)
+        }
+        w_sb = {i: held.tile([P, width[i] // P, M], BF16, name="w%d_sb" % i) for i in (1, 2)}
+        w0_sb = held.tile([P, M], BF16, name="w0_sb")
+        words = held.tile([P, SB, D], BF16, name="words")
+        bias = {i: held.tile([P, MB], F32, name="bias%d" % i) for i in (0, 1, 2)}
+        wa_col = held.tile([P, MB], BF16, name="wa_col")
+
+        def load_x(i, q):
+            nc.sync.dma_start(x_sb[i, q][:], x_dram[i][:, :, q * W : (q + 1) * W])
+
+        load_x(1, 0)
+        table_blocks = table.rearrange("(b p) d -> p b d", p=P)
+        for g in range(SB // TURNED):
+            nc.sync.dma_start(
+                words[:, g * TURNED : (g + 1) * TURNED, :], table_blocks[:, g * TURNED : (g + 1) * TURNED, :]
+            )
+        load_x(2, 0)
+        for q in range(1, PIECES):
+            load_x(1, q)
+            load_x(2, q)
+
+        nc.scalar.dma_start(w_sb[1][:], w1.rearrange("(k p) m -> p k m", p=P))
+        nc.scalar.dma_start(w0_sb[:], w0)
+        with nc.allow_non_contiguous_dma(reason="one value to a partition: 512 small pieces, once"):
+            nc.scalar.dma_start(bias[1][:], b1.rearrange("(a p) o -> p (a o)", p=P))
+            nc.scalar.dma_start(bias[0][:], b0.rearrange("(a p) o -> p (a o)", p=P))
+            nc.scalar.dma_start(wa_col[:], wa.rearrange("(a p) o -> p (a o)", p=P))
+            nc.scalar.dma_start(bias[2][:], b2.rearrange("(a p) o -> p (a o)", p=P))
+        nc.scalar.dma_start(w_sb[2][:], w2.rearrange("(k p) m -> p k m", p=P))
+
+        identity = held.tile([P, P], BF16, name="identity")
+        make_identity(nc, identity[:])
+        wa_all = held.tile([P, MB, P], BF16, name="wa_all")
+        nc.vector.tensor_copy(wa_all[:], wa_col[:].unsqueeze(2).to_broadcast([P, MB, P]))
+
+        def leave_bank(dest, acc, i, a):
+            nc.scalar.activation(dest, acc[:], ACT.Identity, bias=bias[i][:, a : a + 1])
+
+        def leave_bank_on_vector(dest, acc, i, a):
+            nc.vector.tensor_scalar(dest, acc[:], bias[i][:, a : a + 1], None, ALU.add)
+
+        def project(i, q):
+            p_sb = proj.tile([P, MB, W], BF16, name="p%d_sb" % i)
+            blocks = width[i] // P
+            for a in range(MB):
+                acc = bank.tile([P, W], F32, name="acc")
+                for k in range(blocks):
+                    nc.tensor.matmul(
+                        acc[:],
+                        w_sb[i][:, k, a * P : (a + 1) * P],
+                        x_sb[i, q][:, k, :],
+                        start=(k == 0),
+                        stop=(k == blocks - 1),
+                    )
+                leave_bank(p_sb[:, a, :], acc, i, a)
+            return p_sb
+
+        p1_first = project(1, 0)
+
+        window = held.tile([P, S], BF16, name="window")
+        for g in range(SB // TURNED):
+            turned = turn.tile([P, TURNED * P], BF16, name="turned")
+            for b in range(TURNED):
+                nc.tensor.transpose(turned[:, b * P : (b + 1) * P], words[:, g * TURNED + b, :], identity[:])
+            nc.vector.tensor_copy(window[:, g * TURNED * P : (g + 1) * TURNED * P], turned[:])
+
+        p0_sb = held.tile([P, MB, N], BF16, name="p0_sb")
+        for q in range(PIECES):
+            picked = window[:].indirect(offsets[:, q * (W // 16) : (q + 1) * (W // 16)])
+            for a in range(MB):
+                acc = bank.tile([P, W], F32, name="acc")
+                nc.tensor.matmul(acc[:], w0_sb[:, a * P : (a + 1) * P], picked, start=True, stop=True)
+                if a % 2 == 0:
+                    leave_bank(p0_sb[:, a, q * W : (q + 1) * W], acc, 0, a)
+                else:
+                    leave_bank_on_vector(p0_sb[:, a, q * W : (q + 1) * W], acc, 0, a)
+
+        for q in range(PIECES):
+            p1_sb = p1_first if q == 0 else project(1, q)
+            p2_sb = project(2, q)
+            p_of = {0: p0_sb[:, :, q * W : (q + 1) * W], 1: p1_sb[:], 2: p2_sb[:]}
+
+            logit = {}
+            for i in (0, 1, 2):
+                logit[i] = bank.tile([P, W], F32, name="logit%d" % i, tag="acc")
+                for a in range(MB):
+                    nc.tensor.matmul(
+                        logit[i][:], wa_all[:, a, :], p_of[i][:, a, :], start=(a == 0), stop=(a == MB - 1)
+                    )
+
+            logit0 = soft.tile([P, W], F32, name="logit0_sb")
+            nc.scalar.copy(logit0[:], logit[0][:])
+            top01 = soft.tile([P, W], F32, name="top01")
+            nc.vector.tensor_tensor(top01[:], logit0[:], logit[1][:], ALU.max)
+            top = soft.tile([P, W], F32, name="top")
+            nc.vector.tensor_tensor(top[:], top01[:], logit[2][:], ALU.max)
+            below = soft.tile([P, 3, W], F32, name="below")
+            grown = soft.tile([P, 3, W], F32, name="grown")
+            for i in (0, 1, 2):
+                nc.vector.tensor_tensor(below[:, i, :], logit[i][:], top[:], ALU.subtract)
+                nc.scalar.activation(grown[:, i, :], below[:, i, :], ACT.Exp)
+            sum01 = soft.tile([P, W], F32, name="sum01")
+            nc.vector.tensor_tensor(sum01[:], grown[:, 0, :], grown[:, 1, :], ALU.add)
+            total = soft.tile([P, W], F32, name="total")
+            nc.vector.tensor_tensor(total[:], sum01[:], grown[:, 2, :], ALU.add)
+            inverse = soft.tile([P, W], F32, name="inverse")
+            nc.vector.reciprocal(inverse[:], total[:])
+            share = soft.tile([P, 3, W], F32, name="share")
+            for i in (0, 1, 2):
+                nc.vector.tensor_tensor(share[:, i, :], grown[:, i, :], inverse[:], ALU.mult)
+
+            for a in range(MB):
+                part0 = work.tile([P, W], F32, name="part0")
+                nc.vector.tensor_tensor(part0[:], p_of[0][:, a, :], share[:, 0, :], ALU.mult)
+                part1 = work.tile([P, W], F32, name="part1")
+                nc.vector.tensor_tensor(part1[:], p_of[1][:, a, :], share[:, 1, :], ALU.mult)
+                part2 = work.tile([P, W], F32, name="part2")
+                nc.vector.tensor_tensor(part2[:], p_of[2][:, a, :], share[:, 2, :], ALU.mult)
+                both = work.tile([P, W], F32, name="both")
+                nc.vector.tensor_tensor(both[:], part0[:], part1[:], ALU.add)
+                mixed = work.tile([P, W], F32, name="mixed")
+                nc.vector.tensor_tensor(mixed[:], both[:], part2[:], ALU.add)
+                nc.sync.dma_start(out[a * P : (a + 1) * P, q * W : (q + 1) * W], mixed[:])

@@ -6,14 +6,18 @@ from concourse.masks import make_identity
 BF16, F32, U16 = mybir.dt.bfloat16, mybir.dt.float32, mybir.dt.uint16
 ACT = mybir.ActivationFunctionType
 ALU = mybir.AluOpType
+X = mybir.AxisListType.X
 
 P = 128
 S, D, M, N, E1, E2 = 4096, 128, 512, 2048, 1024, 768
-W = 512
-PIECES = N // W
+CHUNK = 512
+CHUNKS = N // CHUNK
 MB = M // P
 SB = S // P
 TURNED = 8
+SOURCES = (0, 1, 2)
+WIDTHS = (512, 512, 512, 256, 128, 128)
+assert sum(WIDTHS) == N
 
 FLOPS = 2 * M * N * (D + E1 + E2) + 2 * 3 * M * N
 
@@ -24,139 +28,152 @@ def tile_dynamicmetaembedding_b_kernel(tc, table, w0, b0, x1, w1, b1, x2, w2, b2
         held = ctx.enter_context(tc.tile_pool(name="held", bufs=1))
         proj = ctx.enter_context(tc.tile_pool(name="proj", bufs=2))
         soft = ctx.enter_context(tc.tile_pool(name="soft", bufs=2))
-        work = ctx.enter_context(tc.tile_pool(name="work", bufs=3))
-        bank = ctx.enter_context(tc.psum_pool(name="bank", bufs=7))
-        turn = ctx.enter_context(tc.psum_pool(name="turn", bufs=1))
+        work = ctx.enter_context(tc.tile_pool(name="work", bufs=2))
+        bank = ctx.enter_context(tc.psum_pool(name="bank", bufs=5))
+        wide = ctx.enter_context(tc.psum_pool(name="wide", bufs=1))
 
         offsets = held.tile([P, N // 16], U16, name="offsets")
-        nc.sync.dma_start(offsets[:], offs)
-
-        width = {1: E1, 2: E2}
-        x_dram = {1: x1.rearrange("(k p) j -> p k j", p=P), 2: x2.rearrange("(k p) j -> p k j", p=P)}
-        x_sb = {
-            (i, q): held.tile([P, width[i] // P, W], BF16, name="x%d_%d" % (i, q))
-            for i in (1, 2)
-            for q in range(PIECES)
-        }
-        w_sb = {i: held.tile([P, width[i] // P, M], BF16, name="w%d_sb" % i) for i in (1, 2)}
+        words = held.tile([P, SB // TURNED, TURNED, D], BF16, name="words")
         w0_sb = held.tile([P, M], BF16, name="w0_sb")
-        words = held.tile([P, SB, D], BF16, name="words")
-        bias = {i: held.tile([P, MB], F32, name="bias%d" % i) for i in (0, 1, 2)}
+        depth = {1: E1 // P, 2: E2 // P}
+        w_sb = {i: held.tile([P, depth[i], M], BF16, name="w%d_sb" % i) for i in (1, 2)}
+        x_sb = {
+            (i, c): held.tile([P, depth[i], CHUNK], BF16, name="x%d_%d" % (i, c))
+            for i in (1, 2)
+            for c in range(CHUNKS)
+        }
+        bias = {i: held.tile([P, MB], F32, name="bias%d" % i) for i in SOURCES}
         wa_col = held.tile([P, MB], BF16, name="wa_col")
 
-        def load_x(i, q):
-            nc.sync.dma_start(x_sb[i, q][:], x_dram[i][:, :, q * W : (q + 1) * W])
+        table_runs = table.rearrange("(g p r) d -> p g (r d)", p=P, r=TURNED)
+        x_dram = {1: x1.rearrange("(k p) j -> p k j", p=P), 2: x2.rearrange("(k p) j -> p k j", p=P)}
+        w_dram = {1: w1.rearrange("(k p) m -> p k m", p=P), 2: w2.rearrange("(k p) m -> p k m", p=P)}
+        b_dram = {0: b0, 1: b1, 2: b2}
 
-        load_x(1, 0)
-        table_blocks = table.rearrange("(b p) d -> p b d", p=P)
-        for g in range(SB // TURNED):
-            nc.sync.dma_start(
-                words[:, g * TURNED : (g + 1) * TURNED, :], table_blocks[:, g * TURNED : (g + 1) * TURNED, :]
-            )
-        load_x(2, 0)
-        for q in range(1, PIECES):
-            load_x(1, q)
-            load_x(2, q)
+        def load_words(queue, g):
+            queue.dma_start(words[:, g, :, :].rearrange("p r d -> p (r d)"), table_runs[:, g, :])
 
-        nc.scalar.dma_start(w_sb[1][:], w1.rearrange("(k p) m -> p k m", p=P))
+        def load_column(dest, vector):
+            with nc.allow_non_contiguous_dma(reason="one value to a partition: 512 small pieces, once"):
+                nc.gpsimd.dma_start(dest[:], vector.rearrange("(a p) o -> p (a o)", p=P))
+
+        load_words(nc.sync, 0)
+        load_words(nc.scalar, 1)
+        load_words(nc.sync, 2)
+        load_words(nc.scalar, 3)
+        nc.sync.dma_start(offsets[:], offs)
         nc.scalar.dma_start(w0_sb[:], w0)
-        with nc.allow_non_contiguous_dma(reason="one value to a partition: 512 small pieces, once"):
-            nc.scalar.dma_start(bias[1][:], b1.rearrange("(a p) o -> p (a o)", p=P))
-            nc.scalar.dma_start(bias[0][:], b0.rearrange("(a p) o -> p (a o)", p=P))
-            nc.scalar.dma_start(wa_col[:], wa.rearrange("(a p) o -> p (a o)", p=P))
-            nc.scalar.dma_start(bias[2][:], b2.rearrange("(a p) o -> p (a o)", p=P))
-        nc.scalar.dma_start(w_sb[2][:], w2.rearrange("(k p) m -> p k m", p=P))
+        for i in SOURCES:
+            load_column(bias[i], b_dram[i])
+        load_column(wa_col, wa)
+        for i in (1, 2):
+            nc.scalar.dma_start(w_sb[i][:], w_dram[i])
+            nc.sync.dma_start(x_sb[i, 0][:], x_dram[i][:, :, 0:CHUNK])
+        for c in range(1, CHUNKS):
+            for i in (1, 2):
+                nc.sync.dma_start(x_sb[i, c][:], x_dram[i][:, :, c * CHUNK : (c + 1) * CHUNK])
 
         identity = held.tile([P, P], BF16, name="identity")
         make_identity(nc, identity[:])
-        wa_all = held.tile([P, MB, P], BF16, name="wa_all")
-        nc.vector.tensor_copy(wa_all[:], wa_col[:].unsqueeze(2).to_broadcast([P, MB, P]))
+        ones = held.tile([P, P], BF16, name="ones")
+        nc.vector.memset(ones[:], 1.0)
 
-        def leave_bank(dest, acc, i, a):
-            nc.scalar.activation(dest, acc[:], ACT.Identity, bias=bias[i][:, a : a + 1])
-
-        def leave_bank_on_vector(dest, acc, i, a):
-            nc.vector.tensor_scalar(dest, acc[:], bias[i][:, a : a + 1], None, ALU.add)
-
-        def project(i, q):
-            p_sb = proj.tile([P, MB, W], BF16, name="p%d_sb" % i)
-            blocks = width[i] // P
-            for a in range(MB):
-                acc = bank.tile([P, W], F32, name="acc")
-                for k in range(blocks):
-                    nc.tensor.matmul(
-                        acc[:],
-                        w_sb[i][:, k, a * P : (a + 1) * P],
-                        x_sb[i, q][:, k, :],
-                        start=(k == 0),
-                        stop=(k == blocks - 1),
-                    )
-                leave_bank(p_sb[:, a, :], acc, i, a)
-            return p_sb
-
-        p1_first = project(1, 0)
+        def leave_bank(engine, dest, acc, i, a):
+            if engine == "scalar":
+                nc.scalar.activation(dest, acc[:], ACT.Identity, bias=bias[i][:, a : a + 1])
+            else:
+                nc.vector.tensor_scalar(dest, acc[:], bias[i][:, a : a + 1], None, ALU.add)
 
         window = held.tile([P, S], BF16, name="window")
         for g in range(SB // TURNED):
-            turned = turn.tile([P, TURNED * P], BF16, name="turned")
-            for b in range(TURNED):
-                nc.tensor.transpose(turned[:, b * P : (b + 1) * P], words[:, g * TURNED + b, :], identity[:])
-            nc.vector.tensor_copy(window[:, g * TURNED * P : (g + 1) * TURNED * P], turned[:])
+            turned = bank.tile([P, TURNED * P], BF16, name="turned", tag="acc")
+            for r in range(TURNED):
+                nc.tensor.transpose(turned[:, r * P : (r + 1) * P], words[:, g, r, :], identity[:])
+            nc.vector.tensor_copy(
+                window[:, g * TURNED * P : (g + 1) * TURNED * P].rearrange("d (p r) -> d p r", r=TURNED),
+                turned[:].rearrange("d (r p) -> d p r", r=TURNED),
+            )
 
         p0_sb = held.tile([P, MB, N], BF16, name="p0_sb")
-        for q in range(PIECES):
-            picked = window[:].indirect(offsets[:, q * (W // 16) : (q + 1) * (W // 16)])
+        for c in range(CHUNKS):
+            picked = window[:].indirect(offsets[:, c * (CHUNK // 16) : (c + 1) * (CHUNK // 16)])
             for a in range(MB):
-                acc = bank.tile([P, W], F32, name="acc")
+                acc = bank.tile([P, CHUNK], F32, name="acc")
                 nc.tensor.matmul(acc[:], w0_sb[:, a * P : (a + 1) * P], picked, start=True, stop=True)
-                if a % 2 == 0:
-                    leave_bank(p0_sb[:, a, q * W : (q + 1) * W], acc, 0, a)
-                else:
-                    leave_bank_on_vector(p0_sb[:, a, q * W : (q + 1) * W], acc, 0, a)
+                leave_bank("scalar" if a % 2 == 0 else "vector", p0_sb[:, a, c * CHUNK : (c + 1) * CHUNK], acc, 0, a)
 
-        for q in range(PIECES):
-            p1_sb = p1_first if q == 0 else project(1, q)
-            p2_sb = project(2, q)
-            p_of = {0: p0_sb[:, :, q * W : (q + 1) * W], 1: p1_sb[:], 2: p2_sb[:]}
+        out_blocks = out.rearrange("(a p) j -> p a j", p=P)
+        first = 0
+        for width in WIDTHS:
+            tokens = slice(first, first + width)
+            c, inside = first // CHUNK, first % CHUNK
+            groups = width // P
 
-            logit = {}
-            for i in (0, 1, 2):
-                logit[i] = bank.tile([P, W], F32, name="logit%d" % i, tag="acc")
+            def project(i):
+                p_sb = proj.tile([P, MB, width], BF16, name="p%d_sb" % i)
                 for a in range(MB):
-                    nc.tensor.matmul(
-                        logit[i][:], wa_all[:, a, :], p_of[i][:, a, :], start=(a == 0), stop=(a == MB - 1)
-                    )
+                    acc = bank.tile([P, width], F32, name="acc")
+                    for k in range(depth[i]):
+                        nc.tensor.matmul(
+                            acc[:],
+                            w_sb[i][:, k, a * P : (a + 1) * P],
+                            x_sb[i, c][:, k, inside : inside + width],
+                            start=(k == 0),
+                            stop=(k == depth[i] - 1),
+                        )
+                    leave_bank("scalar", p_sb[:, a, :], acc, i, a)
+                return p_sb[:]
 
-            logit0 = soft.tile([P, W], F32, name="logit0_sb")
-            nc.scalar.copy(logit0[:], logit[0][:])
-            top01 = soft.tile([P, W], F32, name="top01")
-            nc.vector.tensor_tensor(top01[:], logit0[:], logit[1][:], ALU.max)
-            top = soft.tile([P, W], F32, name="top")
-            nc.vector.tensor_tensor(top[:], top01[:], logit[2][:], ALU.max)
-            below = soft.tile([P, 3, W], F32, name="below")
-            grown = soft.tile([P, 3, W], F32, name="grown")
-            for i in (0, 1, 2):
-                nc.vector.tensor_tensor(below[:, i, :], logit[i][:], top[:], ALU.subtract)
-                nc.scalar.activation(grown[:, i, :], below[:, i, :], ACT.Exp)
-            sum01 = soft.tile([P, W], F32, name="sum01")
-            nc.vector.tensor_tensor(sum01[:], grown[:, 0, :], grown[:, 1, :], ALU.add)
-            total = soft.tile([P, W], F32, name="total")
-            nc.vector.tensor_tensor(total[:], sum01[:], grown[:, 2, :], ALU.add)
-            inverse = soft.tile([P, W], F32, name="inverse")
+            def score(i, p_i):
+                for g in range(groups):
+                    for a in range(MB):
+                        nc.tensor.matmul(
+                            partial[:, g, i, a : a + 1],
+                            p_i[:, a, g * P : (g + 1) * P],
+                            wa_col[:, a : a + 1],
+                            start=True,
+                            stop=True,
+                        )
+
+            p_of = {0: p0_sb[:, :, tokens], 1: project(1), 2: project(2)}
+            partial = bank.tile([P, groups, len(SOURCES), MB], F32, name="partial", tag="acc")
+            for i in SOURCES:
+                score(i, p_of[i])
+
+            by_source = [P, groups, len(SOURCES)]
+            logit = soft.tile(by_source, F32, name="logit")
+            nc.vector.tensor_reduce(logit[:], partial[:], X, ALU.add)
+            top = soft.tile([P, groups], F32, name="top")
+            nc.vector.tensor_reduce(top[:], logit[:], X, ALU.max)
+            below = soft.tile(by_source, F32, name="below")
+            nc.vector.tensor_tensor(below[:], logit[:], top[:].unsqueeze(2).to_broadcast(by_source), ALU.subtract)
+            grown = soft.tile(by_source, F32, name="grown")
+            nc.scalar.activation(grown[:], below[:], ACT.Exp)
+            total = soft.tile([P, groups], F32, name="total")
+            nc.vector.tensor_reduce(total[:], grown[:], X, ALU.add)
+            inverse = soft.tile([P, groups], F32, name="inverse")
             nc.vector.reciprocal(inverse[:], total[:])
-            share = soft.tile([P, 3, W], F32, name="share")
-            for i in (0, 1, 2):
-                nc.vector.tensor_tensor(share[:, i, :], grown[:, i, :], inverse[:], ALU.mult)
+            share = soft.tile(by_source, F32, name="share")
+            nc.vector.tensor_tensor(share[:], grown[:], inverse[:].unsqueeze(2).to_broadcast(by_source), ALU.mult)
 
-            for a in range(MB):
-                part0 = work.tile([P, W], F32, name="part0")
-                nc.vector.tensor_tensor(part0[:], p_of[0][:, a, :], share[:, 0, :], ALU.mult)
-                part1 = work.tile([P, W], F32, name="part1")
-                nc.vector.tensor_tensor(part1[:], p_of[1][:, a, :], share[:, 1, :], ALU.mult)
-                part2 = work.tile([P, W], F32, name="part2")
-                nc.vector.tensor_tensor(part2[:], p_of[2][:, a, :], share[:, 2, :], ALU.mult)
-                both = work.tile([P, W], F32, name="both")
-                nc.vector.tensor_tensor(both[:], part0[:], part1[:], ALU.add)
-                mixed = work.tile([P, W], F32, name="mixed")
-                nc.vector.tensor_tensor(mixed[:], both[:], part2[:], ALU.add)
-                nc.sync.dma_start(out[a * P : (a + 1) * P, q * W : (q + 1) * W], mixed[:])
+            spread = soft.tile([P, len(SOURCES), width], BF16, name="spread")
+            att = {}
+            for i in SOURCES:
+                for g in range(groups):
+                    nc.vector.tensor_scalar(
+                        spread[:, i, g * P : (g + 1) * P], identity[:], share[:, g, i : i + 1], None, ALU.mult
+                    )
+                att[i] = wide.tile([P, width], BF16, name="att%d" % i)
+                nc.tensor.matmul(att[i][:], ones[:], spread[:, i, :], start=True, stop=True)
+
+            whole = [P, MB, width]
+            part = {}
+            for i in SOURCES:
+                part[i] = work.tile(whole, BF16, name="part%d" % i)
+                nc.vector.tensor_tensor(part[i][:], p_of[i], att[i][:].unsqueeze(1).to_broadcast(whole), ALU.mult)
+            both = work.tile(whole, BF16, name="both")
+            nc.vector.tensor_tensor(both[:], part[0][:], part[1][:], ALU.add)
+            mixed = work.tile(whole, F32, name="mixed")
+            nc.vector.tensor_tensor(mixed[:], both[:], part[2][:], ALU.add)
+            nc.sync.dma_start(out_blocks[:, :, tokens], mixed[:])
+            first += width

@@ -14,7 +14,7 @@ CHUNK = 512
 CHUNKS = N // CHUNK
 MB = M // P
 SB = S // P
-TURNED = 8
+TURNED = 4
 SOURCES = (0, 1, 2)
 WIDTHS = (512, 512, 512, 256, 128, 128)
 assert sum(WIDTHS) == N
@@ -26,7 +26,7 @@ def tile_dynamicmetaembedding_b_kernel(tc, table, w0, b0, x1, w1, b1, x2, w2, b2
     nc = tc.nc
     with ExitStack() as ctx:
         held = ctx.enter_context(tc.tile_pool(name="held", bufs=1))
-        proj = ctx.enter_context(tc.tile_pool(name="proj", bufs=2))
+        proj = ctx.enter_context(tc.tile_pool(name="proj", bufs=3))
         soft = ctx.enter_context(tc.tile_pool(name="soft", bufs=2))
         work = ctx.enter_context(tc.tile_pool(name="work", bufs=2))
         bank = ctx.enter_context(tc.psum_pool(name="bank", bufs=5))
@@ -50,25 +50,21 @@ def tile_dynamicmetaembedding_b_kernel(tc, table, w0, b0, x1, w1, b1, x2, w2, b2
         w_dram = {1: w1.rearrange("(k p) m -> p k m", p=P), 2: w2.rearrange("(k p) m -> p k m", p=P)}
         b_dram = {0: b0, 1: b1, 2: b2}
 
-        def load_words(queue, g):
-            queue.dma_start(words[:, g, :, :].rearrange("p r d -> p (r d)"), table_runs[:, g, :])
 
         def load_column(dest, vector):
             with nc.allow_non_contiguous_dma(reason="one value to a partition: 512 small pieces, once"):
-                nc.gpsimd.dma_start(dest[:], vector.rearrange("(a p) o -> p (a o)", p=P))
+                nc.sync.dma_start(dest[:], vector.rearrange("(a p) o -> p (a o)", p=P))
 
-        load_words(nc.sync, 0)
-        load_words(nc.scalar, 1)
-        load_words(nc.sync, 2)
-        load_words(nc.scalar, 3)
+        for g in range(SB // TURNED):
+            nc.sync.dma_start(words[:, g, :, :].rearrange("p r d -> p (r d)"), table_runs[:, g, :])
         nc.sync.dma_start(offsets[:], offs)
-        nc.scalar.dma_start(w0_sb[:], w0)
-        for i in SOURCES:
+        nc.sync.dma_start(w0_sb[:], w0)
+        load_column(bias[0], b_dram[0])
+        for i in (1, 2):
+            nc.sync.dma_start(w_sb[i][:], w_dram[i])
+            nc.sync.dma_start(x_sb[i, 0][:], x_dram[i][:, :, 0:CHUNK])
             load_column(bias[i], b_dram[i])
         load_column(wa_col, wa)
-        for i in (1, 2):
-            nc.scalar.dma_start(w_sb[i][:], w_dram[i])
-            nc.sync.dma_start(x_sb[i, 0][:], x_dram[i][:, :, 0:CHUNK])
         for c in range(1, CHUNKS):
             for i in (1, 2):
                 nc.sync.dma_start(x_sb[i, c][:], x_dram[i][:, :, c * CHUNK : (c + 1) * CHUNK])
@@ -89,10 +85,12 @@ def tile_dynamicmetaembedding_b_kernel(tc, table, w0, b0, x1, w1, b1, x2, w2, b2
             turned = bank.tile([P, TURNED * P], BF16, name="turned", tag="acc")
             for r in range(TURNED):
                 nc.tensor.transpose(turned[:, r * P : (r + 1) * P], words[:, g, r, :], identity[:])
-            nc.vector.tensor_copy(
-                window[:, g * TURNED * P : (g + 1) * TURNED * P].rearrange("d (p r) -> d p r", r=TURNED),
-                turned[:].rearrange("d (r p) -> d p r", r=TURNED),
-            )
+            in_order = window[:, g * TURNED * P : (g + 1) * TURNED * P].rearrange("d (p r) -> d p r", r=TURNED)
+            as_turned = turned[:].rearrange("d (r p) -> d p r", r=TURNED)
+            if g % 2 == 0:
+                nc.vector.tensor_copy(in_order, as_turned)
+            else:
+                nc.scalar.copy(in_order, as_turned)
 
         p0_sb = held.tile([P, MB, N], BF16, name="p0_sb")
         for c in range(CHUNKS):
@@ -103,77 +101,84 @@ def tile_dynamicmetaembedding_b_kernel(tc, table, w0, b0, x1, w1, b1, x2, w2, b2
                 leave_bank("scalar" if a % 2 == 0 else "vector", p0_sb[:, a, c * CHUNK : (c + 1) * CHUNK], acc, 0, a)
 
         out_blocks = out.rearrange("(a p) j -> p a j", p=P)
-        first = 0
-        for width in WIDTHS:
-            tokens = slice(first, first + width)
+
+        def project(i, first, width):
             c, inside = first // CHUNK, first % CHUNK
+            p_sb = proj.tile([P, MB, width], BF16, name="p%d_sb" % i)
+            for a in range(MB):
+                acc = bank.tile([P, width], F32, name="acc")
+                for k in range(depth[i]):
+                    nc.tensor.matmul(
+                        acc[:],
+                        w_sb[i][:, k, a * P : (a + 1) * P],
+                        x_sb[i, c][:, k, inside : inside + width],
+                        start=(k == 0),
+                        stop=(k == depth[i] - 1),
+                    )
+                leave_bank("scalar", p_sb[:, a, :], acc, i, a)
+            return p_sb[:]
+
+        def weigh(width, p_of):
             groups = width // P
-
-            def project(i):
-                p_sb = proj.tile([P, MB, width], BF16, name="p%d_sb" % i)
-                for a in range(MB):
-                    acc = bank.tile([P, width], F32, name="acc")
-                    for k in range(depth[i]):
-                        nc.tensor.matmul(
-                            acc[:],
-                            w_sb[i][:, k, a * P : (a + 1) * P],
-                            x_sb[i, c][:, k, inside : inside + width],
-                            start=(k == 0),
-                            stop=(k == depth[i] - 1),
-                        )
-                    leave_bank("scalar", p_sb[:, a, :], acc, i, a)
-                return p_sb[:]
-
-            def score(i, p_i):
+            partial = bank.tile([P, groups, len(SOURCES), MB], F32, name="partial", tag="acc")
+            for i in SOURCES:
                 for g in range(groups):
                     for a in range(MB):
                         nc.tensor.matmul(
                             partial[:, g, i, a : a + 1],
-                            p_i[:, a, g * P : (g + 1) * P],
+                            p_of[i][:, a, g * P : (g + 1) * P],
                             wa_col[:, a : a + 1],
                             start=True,
                             stop=True,
                         )
-
-            p_of = {0: p0_sb[:, :, tokens], 1: project(1), 2: project(2)}
-            partial = bank.tile([P, groups, len(SOURCES), MB], F32, name="partial", tag="acc")
-            for i in SOURCES:
-                score(i, p_of[i])
-
             by_source = [P, groups, len(SOURCES)]
             logit = soft.tile(by_source, F32, name="logit")
             nc.vector.tensor_reduce(logit[:], partial[:], X, ALU.add)
-            top = soft.tile([P, groups], F32, name="top")
-            nc.vector.tensor_reduce(top[:], logit[:], X, ALU.max)
-            below = soft.tile(by_source, F32, name="below")
-            nc.vector.tensor_tensor(below[:], logit[:], top[:].unsqueeze(2).to_broadcast(by_source), ALU.subtract)
+            under = soft.tile([P, groups], F32, name="under")
+            nc.vector.tensor_reduce(under[:], logit[:], X, ALU.max, negate=True)
             grown = soft.tile(by_source, F32, name="grown")
-            nc.scalar.activation(grown[:], below[:], ACT.Exp)
             total = soft.tile([P, groups], F32, name="total")
-            nc.vector.tensor_reduce(total[:], grown[:], X, ALU.add)
+            for g in range(groups):
+                nc.scalar.activation(
+                    grown[:, g, :], logit[:, g, :], ACT.Exp, bias=under[:, g : g + 1], accum_out=total[:, g : g + 1]
+                )
             inverse = soft.tile([P, groups], F32, name="inverse")
             nc.vector.reciprocal(inverse[:], total[:])
-            share = soft.tile(by_source, F32, name="share")
-            nc.vector.tensor_tensor(share[:], grown[:], inverse[:].unsqueeze(2).to_broadcast(by_source), ALU.mult)
-
             spread = soft.tile([P, len(SOURCES), width], BF16, name="spread")
-            att = {}
             for i in SOURCES:
                 for g in range(groups):
                     nc.vector.tensor_scalar(
-                        spread[:, i, g * P : (g + 1) * P], identity[:], share[:, g, i : i + 1], None, ALU.mult
+                        spread[:, i, g * P : (g + 1) * P],
+                        identity[:],
+                        grown[:, g, i : i + 1],
+                        inverse[:, g : g + 1],
+                        ALU.mult,
+                        ALU.mult,
                     )
-                att[i] = wide.tile([P, width], BF16, name="att%d" % i)
-                nc.tensor.matmul(att[i][:], ones[:], spread[:, i, :], start=True, stop=True)
+            return spread
 
+        def mix(first, width, p_of, spread):
             whole = [P, MB, width]
             part = {}
             for i in SOURCES:
+                att = wide.tile([P, width], BF16, name="att%d" % i)
+                nc.tensor.matmul(att[:], ones[:], spread[:, i, :], start=True, stop=True)
                 part[i] = work.tile(whole, BF16, name="part%d" % i)
-                nc.vector.tensor_tensor(part[i][:], p_of[i], att[i][:].unsqueeze(1).to_broadcast(whole), ALU.mult)
+                nc.vector.tensor_tensor(part[i][:], p_of[i], att[:].unsqueeze(1).to_broadcast(whole), ALU.mult)
             both = work.tile(whole, BF16, name="both")
             nc.vector.tensor_tensor(both[:], part[0][:], part[1][:], ALU.add)
             mixed = work.tile(whole, F32, name="mixed")
             nc.vector.tensor_tensor(mixed[:], both[:], part[2][:], ALU.add)
-            nc.sync.dma_start(out_blocks[:, :, tokens], mixed[:])
+            nc.sync.dma_start(out_blocks[:, :, first : first + width], mixed[:])
+
+        first = 0
+        weighed = []
+        for width in WIDTHS:
+            p_of = {0: p0_sb[:, :, first : first + width], 1: project(1, first, width), 2: project(2, first, width)}
+            spread = weigh(width, p_of)
+            for earlier in weighed:
+                mix(*earlier)
+            weighed = [(first, width, p_of, spread)]
             first += width
+        for earlier in weighed:
+            mix(*earlier)

@@ -16,7 +16,7 @@ MB = M // P
 SB = S // P
 TURNED = 4
 SOURCES = (0, 1, 2)
-WIDTHS = (512, 512, 512, 256, 128, 128)
+WIDTHS = (256, 256, 256, 256, 256, 256, 256, 128, 128)
 assert sum(WIDTHS) == N
 
 FLOPS = 2 * M * N * (D + E1 + E2) + 2 * 3 * M * N

@@ -48,8 +48,6 @@ def tile_dynamicmetaembedding_b_kernel(tc, table, w0, b0, x1, w1, b1, x2, w2, b2
         table_runs = table.rearrange("(g p r) d -> p g (r d)", p=P, r=TURNED)
         x_dram = {1: x1.rearrange("(k p) j -> p k j", p=P), 2: x2.rearrange("(k p) j -> p k j", p=P)}
         w_dram = {1: w1.rearrange("(k p) m -> p k m", p=P), 2: w2.rearrange("(k p) m -> p k m", p=P)}
-        b_dram = {0: b0, 1: b1, 2: b2}
-
 
         def load_column(dest, vector):
             with nc.allow_non_contiguous_dma(reason="one value to a partition: 512 small pieces, once"):
@@ -59,13 +57,13 @@ def tile_dynamicmetaembedding_b_kernel(tc, table, w0, b0, x1, w1, b1, x2, w2, b2
             nc.sync.dma_start(words[:, g, :, :].rearrange("p r d -> p (r d)"), table_runs[:, g, :])
         nc.sync.dma_start(offsets[:], offs)
         nc.sync.dma_start(w0_sb[:], w0)
-        load_column(bias[0], b_dram[0])
+        load_column(wa_col, wa)
+        load_column(bias[0], b0)
         for i in (1, 2):
             nc.sync.dma_start(w_sb[i][:], w_dram[i])
-            nc.sync.dma_start(x_sb[i, 0][:], x_dram[i][:, :, 0:CHUNK])
-            load_column(bias[i], b_dram[i])
-        load_column(wa_col, wa)
-        for c in range(1, CHUNKS):
+        load_column(bias[1], b1)
+        load_column(bias[2], b2)
+        for c in range(CHUNKS):
             for i in (1, 2):
                 nc.sync.dma_start(x_sb[i, c][:], x_dram[i][:, :, c * CHUNK : (c + 1) * CHUNK])
 
@@ -100,7 +98,86 @@ def tile_dynamicmetaembedding_b_kernel(tc, table, w0, b0, x1, w1, b1, x2, w2, b2
                 nc.tensor.matmul(acc[:], w0_sb[:, a * P : (a + 1) * P], picked, start=True, stop=True)
                 leave_bank("scalar" if a % 2 == 0 else "vector", p0_sb[:, a, c * CHUNK : (c + 1) * CHUNK], acc, 0, a)
 
+        wa_wide = bank.tile([P, M], F32, name="wa_wide", tag="acc")
+        for a in range(MB):
+            nc.tensor.matmul(
+                wa_wide[:, a * P : (a + 1) * P], wa_col[:, a : a + 1].to_broadcast([P, P]), identity[:], start=True, stop=True
+            )
+        wa_row = held.tile([P, M], BF16, name="wa_row")
+        nc.vector.tensor_copy(wa_row[:], wa_wide[:])
+        v_col = {}
+        for i in (1, 2):
+            v_sum = held.tile([P, depth[i]], F32, name="v%d_sum" % i)
+            for k in range(depth[i]):
+                product = work.tile([P, M], F32, name="product")
+                nc.vector.scalar_tensor_tensor(
+                    product[:], w_sb[i][:, k, :], 1.0, wa_row[:], ALU.mult, ALU.mult, accum_out=v_sum[:, k : k + 1]
+                )
+            v_col[i] = held.tile([P, depth[i]], BF16, name="v%d_col" % i)
+            nc.vector.tensor_copy(v_col[i][:], v_sum[:])
+        c_part = held.tile([P, len(SOURCES)], F32, name="c_part")
+        nc.vector.memset(c_part[:], 0.0)
+        for i in (1, 2):
+            small = work.tile([P, MB], F32, name="small")
+            nc.vector.scalar_tensor_tensor(
+                small[:], bias[i][:], 1.0, wa_col[:], ALU.mult, ALU.mult, accum_out=c_part[:, i : i + 1]
+            )
+        c_round = held.tile([P, len(SOURCES)], BF16, name="c_round")
+        nc.vector.tensor_copy(c_round[:], c_part[:])
+        c_bank = bank.tile([P, len(SOURCES)], F32, name="c_bank", tag="acc")
+        nc.tensor.matmul(c_bank[:], ones[:], c_round[:], start=True, stop=True)
+        c_all = held.tile([P, len(SOURCES)], F32, name="c_all")
+        nc.vector.tensor_copy(c_all[:], c_bank[:])
+
         out_blocks = out.rearrange("(a p) j -> p a j", p=P)
+
+        def weigh(first, width):
+            c, inside = first // CHUNK, first % CHUNK
+            groups = width // P
+            by_source = [P, groups, len(SOURCES)]
+            summed = bank.tile(by_source, F32, name="summed", tag="acc")
+            for g in range(groups):
+                for a in range(MB):
+                    nc.tensor.matmul(
+                        summed[:, g, 0:1],
+                        p0_sb[:, a, first + g * P : first + (g + 1) * P],
+                        wa_col[:, a : a + 1],
+                        start=(a == 0),
+                        stop=(a == MB - 1),
+                    )
+                for i in (1, 2):
+                    for k in range(depth[i]):
+                        nc.tensor.matmul(
+                            summed[:, g, i : i + 1],
+                            x_sb[i, c][:, k, inside + g * P : inside + (g + 1) * P],
+                            v_col[i][:, k : k + 1],
+                            start=(k == 0),
+                            stop=(k == depth[i] - 1),
+                        )
+            logit = soft.tile(by_source, F32, name="logit")
+            nc.vector.tensor_tensor(logit[:], summed[:], c_all[:].unsqueeze(1).to_broadcast(by_source), ALU.add)
+            under = soft.tile([P, groups], F32, name="under")
+            nc.vector.tensor_reduce(under[:], logit[:], X, ALU.max, negate=True)
+            grown = soft.tile(by_source, F32, name="grown")
+            total = soft.tile([P, groups], F32, name="total")
+            for g in range(groups):
+                nc.scalar.activation(
+                    grown[:, g, :], logit[:, g, :], ACT.Exp, bias=under[:, g : g + 1], accum_out=total[:, g : g + 1]
+                )
+            inverse = soft.tile([P, groups], F32, name="inverse")
+            nc.vector.reciprocal(inverse[:], total[:])
+            diagonal = soft.tile([P, len(SOURCES), width], BF16, name="diagonal")
+            for i in SOURCES:
+                for g in range(groups):
+                    nc.vector.tensor_scalar(
+                        diagonal[:, i, g * P : (g + 1) * P],
+                        identity[:],
+                        grown[:, g, i : i + 1],
+                        inverse[:, g : g + 1],
+                        ALU.mult,
+                        ALU.mult,
+                    )
+            return diagonal
 
         def project(i, first, width):
             c, inside = first // CHUNK, first % CHUNK
@@ -118,67 +195,32 @@ def tile_dynamicmetaembedding_b_kernel(tc, table, w0, b0, x1, w1, b1, x2, w2, b2
                 leave_bank("scalar", p_sb[:, a, :], acc, i, a)
             return p_sb[:]
 
-        def weigh(width, p_of):
-            groups = width // P
-            partial = bank.tile([P, groups, len(SOURCES), MB], F32, name="partial", tag="acc")
+        def spread(width, diagonal):
+            att = {}
             for i in SOURCES:
-                for g in range(groups):
-                    for a in range(MB):
-                        nc.tensor.matmul(
-                            partial[:, g, i, a : a + 1],
-                            p_of[i][:, a, g * P : (g + 1) * P],
-                            wa_col[:, a : a + 1],
-                            start=True,
-                            stop=True,
-                        )
-            by_source = [P, groups, len(SOURCES)]
-            logit = soft.tile(by_source, F32, name="logit")
-            nc.vector.tensor_reduce(logit[:], partial[:], X, ALU.add)
-            under = soft.tile([P, groups], F32, name="under")
-            nc.vector.tensor_reduce(under[:], logit[:], X, ALU.max, negate=True)
-            grown = soft.tile(by_source, F32, name="grown")
-            total = soft.tile([P, groups], F32, name="total")
-            for g in range(groups):
-                nc.scalar.activation(
-                    grown[:, g, :], logit[:, g, :], ACT.Exp, bias=under[:, g : g + 1], accum_out=total[:, g : g + 1]
-                )
-            inverse = soft.tile([P, groups], F32, name="inverse")
-            nc.vector.reciprocal(inverse[:], total[:])
-            spread = soft.tile([P, len(SOURCES), width], BF16, name="spread")
-            for i in SOURCES:
-                for g in range(groups):
-                    nc.vector.tensor_scalar(
-                        spread[:, i, g * P : (g + 1) * P],
-                        identity[:],
-                        grown[:, g, i : i + 1],
-                        inverse[:, g : g + 1],
-                        ALU.mult,
-                        ALU.mult,
-                    )
-            return spread
+                att[i] = wide.tile([P, width], BF16, name="att%d" % i)
+                nc.tensor.matmul(att[i][:], ones[:], diagonal[:, i, :], start=True, stop=True)
+            return att
 
-        def mix(first, width, p_of, spread):
+        def weighted(i, width, p_i, att):
             whole = [P, MB, width]
-            part = {}
-            for i in SOURCES:
-                att = wide.tile([P, width], BF16, name="att%d" % i)
-                nc.tensor.matmul(att[:], ones[:], spread[:, i, :], start=True, stop=True)
-                part[i] = work.tile(whole, BF16, name="part%d" % i)
-                nc.vector.tensor_tensor(part[i][:], p_of[i], att[:].unsqueeze(1).to_broadcast(whole), ALU.mult)
-            both = work.tile(whole, BF16, name="both")
-            nc.vector.tensor_tensor(both[:], part[0][:], part[1][:], ALU.add)
-            mixed = work.tile(whole, F32, name="mixed")
-            nc.vector.tensor_tensor(mixed[:], both[:], part[2][:], ALU.add)
-            nc.sync.dma_start(out_blocks[:, :, first : first + width], mixed[:])
+            part = work.tile(whole, BF16, name="part%d" % i)
+            nc.vector.tensor_tensor(part[:], p_i, att[i][:].unsqueeze(1).to_broadcast(whole), ALU.mult)
+            return part
 
-        first = 0
-        weighed = []
-        for width in WIDTHS:
-            p_of = {0: p0_sb[:, :, first : first + width], 1: project(1, first, width), 2: project(2, first, width)}
-            spread = weigh(width, p_of)
-            for earlier in weighed:
-                mix(*earlier)
-            weighed = [(first, width, p_of, spread)]
-            first += width
-        for earlier in weighed:
-            mix(*earlier)
+        firsts = [sum(WIDTHS[:u]) for u in range(len(WIDTHS))]
+        diagonal_of = {0: weigh(firsts[0], WIDTHS[0])}
+        for u, (first, width) in enumerate(zip(firsts, WIDTHS)):
+            if u + 1 < len(WIDTHS):
+                diagonal_of[u + 1] = weigh(firsts[u + 1], WIDTHS[u + 1])
+            p1_sb = project(1, first, width)
+            att = spread(width, diagonal_of[u])
+            part0 = weighted(0, width, p0_sb[:, :, first : first + width], att)
+            part1 = weighted(1, width, p1_sb, att)
+            both = work.tile([P, MB, width], BF16, name="both")
+            nc.vector.tensor_tensor(both[:], part0[:], part1[:], ALU.add)
+            p2_sb = project(2, first, width)
+            part2 = weighted(2, width, p2_sb, att)
+            mixed = work.tile([P, MB, width], F32, name="mixed")
+            nc.vector.tensor_tensor(mixed[:], both[:], part2[:], ALU.add)
+            nc.sync.dma_start(out_blocks[:, :, first : first + width], mixed[:])

@@ -6,7 +6,6 @@ from concourse.masks import make_identity
 BF16, F32, U16 = mybir.dt.bfloat16, mybir.dt.float32, mybir.dt.uint16
 ACT = mybir.ActivationFunctionType
 ALU = mybir.AluOpType
-X = mybir.AxisListType.X
 
 P = 128
 S, D, M, N, E1, E2 = 4096, 128, 512, 2048, 1024, 768
@@ -15,6 +14,9 @@ CHUNKS = N // CHUNK
 MB = M // P
 SB = S // P
 TURNED = 4
+QUARTER = 32
+QUARTERS = P // QUARTER
+assert QUARTERS == CHUNKS
 SOURCES = (0, 1, 2)
 WIDTHS = (256, 256, 256, 256, 256, 256, 256, 128, 128)
 assert sum(WIDTHS) == N
@@ -26,16 +28,14 @@ def tile_dynamicmetaembedding_b_kernel(tc, table, w0, b0, x1, w1, b1, x2, w2, b2
     nc = tc.nc
     with ExitStack() as ctx:
         held = ctx.enter_context(tc.tile_pool(name="held", bufs=1))
-        proj = ctx.enter_context(tc.tile_pool(name="proj", bufs=3))
-        soft = ctx.enter_context(tc.tile_pool(name="soft", bufs=2))
+        proj = ctx.enter_context(tc.tile_pool(name="proj", bufs=4))
         work = ctx.enter_context(tc.tile_pool(name="work", bufs=2))
-        bank = ctx.enter_context(tc.psum_pool(name="bank", bufs=5))
-        wide = ctx.enter_context(tc.psum_pool(name="wide", bufs=1))
+        bank = ctx.enter_context(tc.psum_pool(name="bank", bufs=8))
 
         offsets = held.tile([P, N // 16], U16, name="offsets")
         words = held.tile([P, SB // TURNED, TURNED, D], BF16, name="words")
         w0_sb = held.tile([P, M], BF16, name="w0_sb")
-        depth = {1: E1 // P, 2: E2 // P}
+        depth = {0: MB, 1: E1 // P, 2: E2 // P}
         w_sb = {i: held.tile([P, depth[i], M], BF16, name="w%d_sb" % i) for i in (1, 2)}
         x_sb = {
             (i, c): held.tile([P, depth[i], CHUNK], BF16, name="x%d_%d" % (i, c))
@@ -53,18 +53,17 @@ def tile_dynamicmetaembedding_b_kernel(tc, table, w0, b0, x1, w1, b1, x2, w2, b2
             with nc.allow_non_contiguous_dma(reason="one value to a partition: 512 small pieces, once"):
                 nc.sync.dma_start(dest[:], vector.rearrange("(a p) o -> p (a o)", p=P))
 
+        load_column(wa_col, wa)
         for g in range(SB // TURNED):
             nc.sync.dma_start(words[:, g, :, :].rearrange("p r d -> p (r d)"), table_runs[:, g, :])
         nc.sync.dma_start(offsets[:], offs)
         nc.sync.dma_start(w0_sb[:], w0)
-        load_column(wa_col, wa)
         load_column(bias[0], b0)
+        b_dram = {1: b1, 2: b2}
         for i in (1, 2):
             nc.sync.dma_start(w_sb[i][:], w_dram[i])
-        load_column(bias[1], b1)
-        load_column(bias[2], b2)
-        for c in range(CHUNKS):
-            for i in (1, 2):
+            load_column(bias[i], b_dram[i])
+            for c in range(CHUNKS):
                 nc.sync.dma_start(x_sb[i, c][:], x_dram[i][:, :, c * CHUNK : (c + 1) * CHUNK])
 
         identity = held.tile([P, P], BF16, name="identity")
@@ -77,6 +76,14 @@ def tile_dynamicmetaembedding_b_kernel(tc, table, w0, b0, x1, w1, b1, x2, w2, b2
                 nc.scalar.activation(dest, acc[:], ACT.Identity, bias=bias[i][:, a : a + 1])
             else:
                 nc.vector.tensor_scalar(dest, acc[:], bias[i][:, a : a + 1], None, ALU.add)
+
+        wa_wide = bank.tile([P, M], F32, name="wa_wide", tag="acc")
+        for a in range(MB):
+            nc.tensor.matmul(
+                wa_wide[:, a * P : (a + 1) * P], wa_col[:, a : a + 1].to_broadcast([P, P]), identity[:], start=True, stop=True
+            )
+        wa_row = held.tile([P, M], BF16, name="wa_row")
+        nc.vector.tensor_copy(wa_row[:], wa_wide[:])
 
         window = held.tile([P, S], BF16, name="window")
         for g in range(SB // TURNED):
@@ -98,14 +105,7 @@ def tile_dynamicmetaembedding_b_kernel(tc, table, w0, b0, x1, w1, b1, x2, w2, b2
                 nc.tensor.matmul(acc[:], w0_sb[:, a * P : (a + 1) * P], picked, start=True, stop=True)
                 leave_bank("scalar" if a % 2 == 0 else "vector", p0_sb[:, a, c * CHUNK : (c + 1) * CHUNK], acc, 0, a)
 
-        wa_wide = bank.tile([P, M], F32, name="wa_wide", tag="acc")
-        for a in range(MB):
-            nc.tensor.matmul(
-                wa_wide[:, a * P : (a + 1) * P], wa_col[:, a : a + 1].to_broadcast([P, P]), identity[:], start=True, stop=True
-            )
-        wa_row = held.tile([P, M], BF16, name="wa_row")
-        nc.vector.tensor_copy(wa_row[:], wa_wide[:])
-        v_col = {}
+        v_col = {0: wa_col}
         for i in (1, 2):
             v_sum = held.tile([P, depth[i]], F32, name="v%d_sum" % i)
             for k in range(depth[i]):
@@ -115,73 +115,15 @@ def tile_dynamicmetaembedding_b_kernel(tc, table, w0, b0, x1, w1, b1, x2, w2, b2
                 )
             v_col[i] = held.tile([P, depth[i]], BF16, name="v%d_col" % i)
             nc.vector.tensor_copy(v_col[i][:], v_sum[:])
-        c_part = held.tile([P, len(SOURCES)], F32, name="c_part")
-        nc.vector.memset(c_part[:], 0.0)
-        for i in (1, 2):
-            small = work.tile([P, MB], F32, name="small")
-            nc.vector.scalar_tensor_tensor(
-                small[:], bias[i][:], 1.0, wa_col[:], ALU.mult, ALU.mult, accum_out=c_part[:, i : i + 1]
-            )
-        c_round = held.tile([P, len(SOURCES)], BF16, name="c_round")
-        nc.vector.tensor_copy(c_round[:], c_part[:])
-        c_bank = bank.tile([P, len(SOURCES)], F32, name="c_bank", tag="acc")
-        nc.tensor.matmul(c_bank[:], ones[:], c_round[:], start=True, stop=True)
-        c_all = held.tile([P, len(SOURCES)], F32, name="c_all")
-        nc.vector.tensor_copy(c_all[:], c_bank[:])
 
-        out_blocks = out.rearrange("(a p) j -> p a j", p=P)
+        def leave_in_turn(n, dest, filled):
+            if n % 2 == 0:
+                nc.scalar.copy(dest, filled[:])
+            else:
+                nc.vector.tensor_copy(dest, filled[:])
 
-        def weigh(first, width):
+        def project(i, first, width, dest):
             c, inside = first // CHUNK, first % CHUNK
-            groups = width // P
-            by_source = [P, groups, len(SOURCES)]
-            summed = bank.tile(by_source, F32, name="summed", tag="acc")
-            for g in range(groups):
-                for a in range(MB):
-                    nc.tensor.matmul(
-                        summed[:, g, 0:1],
-                        p0_sb[:, a, first + g * P : first + (g + 1) * P],
-                        wa_col[:, a : a + 1],
-                        start=(a == 0),
-                        stop=(a == MB - 1),
-                    )
-                for i in (1, 2):
-                    for k in range(depth[i]):
-                        nc.tensor.matmul(
-                            summed[:, g, i : i + 1],
-                            x_sb[i, c][:, k, inside + g * P : inside + (g + 1) * P],
-                            v_col[i][:, k : k + 1],
-                            start=(k == 0),
-                            stop=(k == depth[i] - 1),
-                        )
-            logit = soft.tile(by_source, F32, name="logit")
-            nc.vector.tensor_tensor(logit[:], summed[:], c_all[:].unsqueeze(1).to_broadcast(by_source), ALU.add)
-            under = soft.tile([P, groups], F32, name="under")
-            nc.vector.tensor_reduce(under[:], logit[:], X, ALU.max, negate=True)
-            grown = soft.tile(by_source, F32, name="grown")
-            total = soft.tile([P, groups], F32, name="total")
-            for g in range(groups):
-                nc.scalar.activation(
-                    grown[:, g, :], logit[:, g, :], ACT.Exp, bias=under[:, g : g + 1], accum_out=total[:, g : g + 1]
-                )
-            inverse = soft.tile([P, groups], F32, name="inverse")
-            nc.vector.reciprocal(inverse[:], total[:])
-            diagonal = soft.tile([P, len(SOURCES), width], BF16, name="diagonal")
-            for i in SOURCES:
-                for g in range(groups):
-                    nc.vector.tensor_scalar(
-                        diagonal[:, i, g * P : (g + 1) * P],
-                        identity[:],
-                        grown[:, g, i : i + 1],
-                        inverse[:, g : g + 1],
-                        ALU.mult,
-                        ALU.mult,
-                    )
-            return diagonal
-
-        def project(i, first, width):
-            c, inside = first // CHUNK, first % CHUNK
-            p_sb = proj.tile([P, MB, width], BF16, name="p%d_sb" % i)
             for a in range(MB):
                 acc = bank.tile([P, width], F32, name="acc")
                 for k in range(depth[i]):
@@ -192,35 +134,90 @@ def tile_dynamicmetaembedding_b_kernel(tc, table, w0, b0, x1, w1, b1, x2, w2, b2
                         start=(k == 0),
                         stop=(k == depth[i] - 1),
                     )
-                leave_bank("scalar", p_sb[:, a, :], acc, i, a)
-            return p_sb[:]
+                leave_bank("scalar", dest[:, a, :], acc, i, a)
 
-        def spread(width, diagonal):
-            att = {}
+        def weigh():
+            c_part = held.tile([P, len(SOURCES)], F32, name="c_part")
+            nc.vector.memset(c_part[:], 0.0)
+            for i in (1, 2):
+                small = work.tile([P, MB], F32, name="small")
+                nc.vector.scalar_tensor_tensor(
+                    small[:], bias[i][:], 1.0, wa_col[:], ALU.mult, ALU.mult, accum_out=c_part[:, i : i + 1]
+                )
+            c_round = held.tile([P, len(SOURCES)], BF16, name="c_round")
+            nc.vector.tensor_copy(c_round[:], c_part[:])
+            c_bank = bank.tile([P, len(SOURCES)], F32, name="c_bank", tag="acc")
+            nc.tensor.matmul(c_bank[:], ones[:], c_round[:], start=True, stop=True)
+            c_all = held.tile([P, len(SOURCES)], F32, name="c_all")
+            nc.vector.tensor_copy(c_all[:], c_bank[:])
+            by_source = [P, len(SOURCES), CHUNK]
+            logit = held.tile(by_source, F32, name="logit")
             for i in SOURCES:
-                att[i] = wide.tile([P, width], BF16, name="att%d" % i)
-                nc.tensor.matmul(att[i][:], ones[:], diagonal[:, i, :], start=True, stop=True)
+                rows = bank.tile([P, CHUNK], F32, name="rows", tag="acc")
+                for k in range(depth[i]):
+                    for q in range(QUARTERS):
+                        nc.tensor.matmul(
+                            rows[q * QUARTER : (q + 1) * QUARTER, :],
+                            v_col[i][:, k : k + 1].to_broadcast([P, QUARTER]),
+                            p0_sb[:, k, q * CHUNK : (q + 1) * CHUNK] if i == 0 else x_sb[i, q][:, k, :],
+                            start=(k == 0),
+                            stop=(k == depth[i] - 1),
+                        )
+                nc.scalar.activation(logit[:, i, :], rows[:], ACT.Identity, bias=c_all[:, i : i + 1])
+            top = held.tile([P, CHUNK], F32, name="top")
+            nc.vector.tensor_tensor(top[:], logit[:, 0, :], logit[:, 1, :], ALU.max)
+            nc.vector.tensor_tensor(top[:], top[:], logit[:, 2, :], ALU.max)
+            below = held.tile(by_source, F32, name="below")
+            nc.vector.tensor_tensor(below[:], logit[:], top[:].unsqueeze(1).to_broadcast(by_source), ALU.subtract)
+            grown = held.tile(by_source, F32, name="grown")
+            nc.scalar.activation(grown[:], below[:], ACT.Exp)
+            total = held.tile([P, CHUNK], F32, name="total")
+            nc.vector.tensor_tensor(total[:], grown[:, 0, :], grown[:, 1, :], ALU.add)
+            nc.vector.tensor_tensor(total[:], total[:], grown[:, 2, :], ALU.add)
+            inverse = held.tile([P, CHUNK], F32, name="inverse")
+            nc.vector.reciprocal(inverse[:], total[:])
+            share = held.tile(by_source, BF16, name="share")
+            nc.vector.tensor_tensor(share[:], grown[:], inverse[:].unsqueeze(1).to_broadcast(by_source), ALU.mult)
+            return share
+
+        def spread(share):
+            att = held.tile([P, len(SOURCES), N], BF16, name="att")
+            for q in range(QUARTERS):
+                pick = identity[:, q * QUARTER : q * QUARTER + 1].to_broadcast([P, P])
+                for i in SOURCES:
+                    picked_row = bank.tile([P, CHUNK], BF16, name="picked_row", tag="acc")
+                    nc.tensor.matmul(picked_row[:], pick, share[:, i, :], start=True, stop=True)
+                    leave_in_turn(q * len(SOURCES) + i, att[:, i, q * CHUNK : (q + 1) * CHUNK], picked_row)
             return att
 
-        def weighted(i, width, p_i, att):
+        def weighted(i, p_i, first, width, att):
             whole = [P, MB, width]
             part = work.tile(whole, BF16, name="part%d" % i)
-            nc.vector.tensor_tensor(part[:], p_i, att[i][:].unsqueeze(1).to_broadcast(whole), ALU.mult)
+            nc.vector.tensor_tensor(part[:], p_i, att[:, i, first : first + width].unsqueeze(1).to_broadcast(whole), ALU.mult)
             return part
 
-        firsts = [sum(WIDTHS[:u]) for u in range(len(WIDTHS))]
-        diagonal_of = {0: weigh(firsts[0], WIDTHS[0])}
-        for u, (first, width) in enumerate(zip(firsts, WIDTHS)):
-            if u + 1 < len(WIDTHS):
-                diagonal_of[u + 1] = weigh(firsts[u + 1], WIDTHS[u + 1])
-            p1_sb = project(1, first, width)
-            att = spread(width, diagonal_of[u])
-            part0 = weighted(0, width, p0_sb[:, :, first : first + width], att)
-            part1 = weighted(1, width, p1_sb, att)
-            both = work.tile([P, MB, width], BF16, name="both")
-            nc.vector.tensor_tensor(both[:], part0[:], part1[:], ALU.add)
-            p2_sb = project(2, first, width)
-            part2 = weighted(2, width, p2_sb, att)
+        p1_sb = held.tile([P, MB, N], BF16, name="p1_sb")
+        for c in range(CHUNKS):
+            project(1, c * CHUNK, CHUNK, p1_sb[:, :, c * CHUNK : (c + 1) * CHUNK])
+            if c == 0:
+                share = weigh()
+            if c == 2:
+                att = spread(share)
+
+        both = held.tile([P, MB, N], BF16, name="both")
+        for c in range(CHUNKS):
+            here = slice(c * CHUNK, (c + 1) * CHUNK)
+            part0 = weighted(0, p0_sb[:, :, here], c * CHUNK, CHUNK, att)
+            part1 = weighted(1, p1_sb[:, :, here], c * CHUNK, CHUNK, att)
+            nc.vector.tensor_tensor(both[:, :, here], part0[:], part1[:], ALU.add)
+
+        out_blocks = out.rearrange("(a p) j -> p a j", p=P)
+        first = 0
+        for width in WIDTHS:
+            p2_sb = proj.tile([P, MB, width], BF16, name="p2_sb")
+            project(2, first, width, p2_sb)
+            part2 = weighted(2, p2_sb[:], first, width, att)
             mixed = work.tile([P, MB, width], F32, name="mixed")
-            nc.vector.tensor_tensor(mixed[:], both[:], part2[:], ALU.add)
+            nc.vector.tensor_tensor(mixed[:], both[:, :, first : first + width], part2[:], ALU.add)
             nc.sync.dma_start(out_blocks[:, :, first : first + width], mixed[:])
+            first += width

@@ -16,10 +16,11 @@ SB = S // P
 TURNED = 4
 QUARTER = 32
 QUARTERS = P // QUARTER
-assert QUARTERS == CHUNKS
+SPAN = 256
+BATCH = QUARTERS * SPAN
 SOURCES = (0, 1, 2)
-WIDTHS = (256, 256, 256, 256, 256, 256, 256, 128, 128)
-assert sum(WIDTHS) == N
+WIDTHS = ((256, 256, 256, 256), (256, 256, 256, 128, 128))
+assert all(sum(widths) == BATCH for widths in WIDTHS) and len(WIDTHS) * BATCH == N
 
 FLOPS = 2 * M * N * (D + E1 + E2) + 2 * 3 * M * N
 
@@ -29,6 +30,7 @@ def tile_dynamicmetaembedding_b_kernel(tc, table, w0, b0, x1, w1, b1, x2, w2, b2
     with ExitStack() as ctx:
         held = ctx.enter_context(tc.tile_pool(name="held", bufs=1))
         proj = ctx.enter_context(tc.tile_pool(name="proj", bufs=4))
+        soft = ctx.enter_context(tc.tile_pool(name="soft", bufs=2))
         work = ctx.enter_context(tc.tile_pool(name="work", bufs=2))
         bank = ctx.enter_context(tc.psum_pool(name="bank", bufs=8))
 
@@ -59,11 +61,12 @@ def tile_dynamicmetaembedding_b_kernel(tc, table, w0, b0, x1, w1, b1, x2, w2, b2
         nc.sync.dma_start(offsets[:], offs)
         nc.sync.dma_start(w0_sb[:], w0)
         load_column(bias[0], b0)
-        b_dram = {1: b1, 2: b2}
         for i in (1, 2):
             nc.sync.dma_start(w_sb[i][:], w_dram[i])
-            load_column(bias[i], b_dram[i])
-            for c in range(CHUNKS):
+        load_column(bias[1], b1)
+        load_column(bias[2], b2)
+        for c in range(CHUNKS):
+            for i in (1, 2):
                 nc.sync.dma_start(x_sb[i, c][:], x_dram[i][:, :, c * CHUNK : (c + 1) * CHUNK])
 
         identity = held.tile([P, P], BF16, name="identity")
@@ -116,12 +119,6 @@ def tile_dynamicmetaembedding_b_kernel(tc, table, w0, b0, x1, w1, b1, x2, w2, b2
             v_col[i] = held.tile([P, depth[i]], BF16, name="v%d_col" % i)
             nc.vector.tensor_copy(v_col[i][:], v_sum[:])
 
-        def leave_in_turn(n, dest, filled):
-            if n % 2 == 0:
-                nc.scalar.copy(dest, filled[:])
-            else:
-                nc.vector.tensor_copy(dest, filled[:])
-
         def project(i, first, width, dest):
             c, inside = first // CHUNK, first % CHUNK
             for a in range(MB):
@@ -136,7 +133,7 @@ def tile_dynamicmetaembedding_b_kernel(tc, table, w0, b0, x1, w1, b1, x2, w2, b2
                     )
                 leave_bank("scalar", dest[:, a, :], acc, i, a)
 
-        def weigh():
+        def constants():
             c_part = held.tile([P, len(SOURCES)], F32, name="c_part")
             nc.vector.memset(c_part[:], 0.0)
             for i in (1, 2):
@@ -150,74 +147,98 @@ def tile_dynamicmetaembedding_b_kernel(tc, table, w0, b0, x1, w1, b1, x2, w2, b2
             nc.tensor.matmul(c_bank[:], ones[:], c_round[:], start=True, stop=True)
             c_all = held.tile([P, len(SOURCES)], F32, name="c_all")
             nc.vector.tensor_copy(c_all[:], c_bank[:])
-            by_source = [P, len(SOURCES), CHUNK]
-            logit = held.tile(by_source, F32, name="logit")
+            return c_all
+
+        def summed_over(i, k, first, width):
+            if i == 0:
+                return p0_sb[:, k, first : first + width]
+            c, inside = first // CHUNK, first % CHUNK
+            return x_sb[i, c][:, k, inside : inside + width]
+
+        def weigh(t, c_all):
+            by_source = [P, len(SOURCES), SPAN]
+            logit = soft.tile(by_source, F32, name="logit")
             for i in SOURCES:
-                rows = bank.tile([P, CHUNK], F32, name="rows", tag="acc")
+                rows = bank.tile([P, SPAN], F32, name="rows", tag="acc")
                 for k in range(depth[i]):
                     for q in range(QUARTERS):
                         nc.tensor.matmul(
                             rows[q * QUARTER : (q + 1) * QUARTER, :],
                             v_col[i][:, k : k + 1].to_broadcast([P, QUARTER]),
-                            p0_sb[:, k, q * CHUNK : (q + 1) * CHUNK] if i == 0 else x_sb[i, q][:, k, :],
+                            summed_over(i, k, t * BATCH + q * SPAN, SPAN),
                             start=(k == 0),
                             stop=(k == depth[i] - 1),
                         )
                 nc.scalar.activation(logit[:, i, :], rows[:], ACT.Identity, bias=c_all[:, i : i + 1])
-            top = held.tile([P, CHUNK], F32, name="top")
+            top = soft.tile([P, SPAN], F32, name="top")
             nc.vector.tensor_tensor(top[:], logit[:, 0, :], logit[:, 1, :], ALU.max)
             nc.vector.tensor_tensor(top[:], top[:], logit[:, 2, :], ALU.max)
-            below = held.tile(by_source, F32, name="below")
+            below = soft.tile(by_source, F32, name="below")
             nc.vector.tensor_tensor(below[:], logit[:], top[:].unsqueeze(1).to_broadcast(by_source), ALU.subtract)
-            grown = held.tile(by_source, F32, name="grown")
+            grown = soft.tile(by_source, F32, name="grown")
             nc.scalar.activation(grown[:], below[:], ACT.Exp)
-            total = held.tile([P, CHUNK], F32, name="total")
+            total = soft.tile([P, SPAN], F32, name="total")
             nc.vector.tensor_tensor(total[:], grown[:, 0, :], grown[:, 1, :], ALU.add)
             nc.vector.tensor_tensor(total[:], total[:], grown[:, 2, :], ALU.add)
-            inverse = held.tile([P, CHUNK], F32, name="inverse")
+            inverse = soft.tile([P, SPAN], F32, name="inverse")
             nc.vector.reciprocal(inverse[:], total[:])
-            share = held.tile(by_source, BF16, name="share")
+            share = soft.tile(by_source, BF16, name="share")
             nc.vector.tensor_tensor(share[:], grown[:], inverse[:].unsqueeze(1).to_broadcast(by_source), ALU.mult)
             return share
 
-        def spread(share):
-            att = held.tile([P, len(SOURCES), N], BF16, name="att")
+        att = held.tile([P, len(SOURCES), N], BF16, name="att")
+
+        def spread(t, share):
             for q in range(QUARTERS):
                 pick = identity[:, q * QUARTER : q * QUARTER + 1].to_broadcast([P, P])
+                first = t * BATCH + q * SPAN
                 for i in SOURCES:
-                    picked_row = bank.tile([P, CHUNK], BF16, name="picked_row", tag="acc")
+                    picked_row = bank.tile([P, SPAN], BF16, name="picked_row", tag="acc")
                     nc.tensor.matmul(picked_row[:], pick, share[:, i, :], start=True, stop=True)
-                    leave_in_turn(q * len(SOURCES) + i, att[:, i, q * CHUNK : (q + 1) * CHUNK], picked_row)
-            return att
+                    nc.scalar.copy(att[:, i, first : first + SPAN], picked_row[:])
 
-        def weighted(i, p_i, first, width, att):
+        def weighted(i, p_i, first, width):
             whole = [P, MB, width]
             part = work.tile(whole, BF16, name="part%d" % i)
             nc.vector.tensor_tensor(part[:], p_i, att[:, i, first : first + width].unsqueeze(1).to_broadcast(whole), ALU.mult)
             return part
 
         p1_sb = held.tile([P, MB, N], BF16, name="p1_sb")
-        for c in range(CHUNKS):
-            project(1, c * CHUNK, CHUNK, p1_sb[:, :, c * CHUNK : (c + 1) * CHUNK])
-            if c == 0:
-                share = weigh()
-            if c == 2:
-                att = spread(share)
-
         both = held.tile([P, MB, N], BF16, name="both")
-        for c in range(CHUNKS):
+        out_blocks = out.rearrange("(a p) j -> p a j", p=P)
+
+        def first_source(c):
+            project(1, c * CHUNK, CHUNK, p1_sb[:, :, c * CHUNK : (c + 1) * CHUNK])
+
+        def two_sources(c):
             here = slice(c * CHUNK, (c + 1) * CHUNK)
-            part0 = weighted(0, p0_sb[:, :, here], c * CHUNK, CHUNK, att)
-            part1 = weighted(1, p1_sb[:, :, here], c * CHUNK, CHUNK, att)
+            part0 = weighted(0, p0_sb[:, :, here], c * CHUNK, CHUNK)
+            part1 = weighted(1, p1_sb[:, :, here], c * CHUNK, CHUNK)
             nc.vector.tensor_tensor(both[:, :, here], part0[:], part1[:], ALU.add)
 
-        out_blocks = out.rearrange("(a p) j -> p a j", p=P)
-        first = 0
-        for width in WIDTHS:
-            p2_sb = proj.tile([P, MB, width], BF16, name="p2_sb")
-            project(2, first, width, p2_sb)
-            part2 = weighted(2, p2_sb[:], first, width, att)
-            mixed = work.tile([P, MB, width], F32, name="mixed")
-            nc.vector.tensor_tensor(mixed[:], both[:, :, first : first + width], part2[:], ALU.add)
-            nc.sync.dma_start(out_blocks[:, :, first : first + width], mixed[:])
-            first += width
+        def last_source(t):
+            first = t * BATCH
+            for width in WIDTHS[t]:
+                p2_sb = proj.tile([P, MB, width], BF16, name="p2_sb")
+                project(2, first, width, p2_sb)
+                part2 = weighted(2, p2_sb[:], first, width)
+                mixed = proj.tile([P, MB, width], F32, name="mixed")
+                nc.vector.tensor_tensor(mixed[:], both[:, :, first : first + width], part2[:], ALU.add)
+                nc.sync.dma_start(out_blocks[:, :, first : first + width], mixed[:])
+                first += width
+
+        first_source(0)
+        c_all = constants()
+        share = weigh(0, c_all)
+        first_source(1)
+        spread(0, share)
+        two_sources(0)
+        two_sources(1)
+        share = weigh(1, c_all)
+        last_source(0)
+        spread(1, share)
+        first_source(2)
+        two_sources(2)
+        first_source(3)
+        two_sources(3)
+        last_source(1)

@@ -188,14 +188,15 @@ def tile_dynamicmetaembedding_b_kernel(tc, table, w0, b0, x1, w1, b1, x2, w2, b2
 
         att = held.tile([P, len(SOURCES), N], BF16, name="att")
 
+        parked = out[0 : len(SOURCES), N - BATCH : N].bitcast(BF16)
+
         def spread(t, share):
             for q in range(QUARTERS):
-                pick = identity[:, q * QUARTER : q * QUARTER + 1].to_broadcast([P, P])
                 first = t * BATCH + q * SPAN
-                for i in SOURCES:
-                    picked_row = bank.tile([P, SPAN], BF16, name="picked_row", tag="acc")
-                    nc.tensor.matmul(picked_row[:], pick, share[:, i, :], start=True, stop=True)
-                    nc.scalar.copy(att[:, i, first : first + SPAN], picked_row[:])
+                nc.sync.dma_start(parked[:, first : first + SPAN].unsqueeze(0), share[q * QUARTER : q * QUARTER + 1, :, :])
+            for i in SOURCES:
+                batch = slice(t * BATCH, (t + 1) * BATCH)
+                nc.sync.dma_start(att[:, i, batch], parked[i, batch].partition_broadcast(P))
 
         def weighted(i, p_i, first, width):
             whole = [P, MB, width]

@@ -61,12 +61,12 @@ def tile_dynamicmetaembedding_b_kernel(tc, table, w0, b0, x1, w1, b1, x2, w2, b2
         nc.sync.dma_start(offsets[:], offs)
         nc.sync.dma_start(w0_sb[:], w0)
         load_column(bias[0], b0)
-        for i in (1, 2):
+        for i in (2, 1):
             nc.sync.dma_start(w_sb[i][:], w_dram[i])
-        load_column(bias[1], b1)
         load_column(bias[2], b2)
+        load_column(bias[1], b1)
         for c in range(CHUNKS):
-            for i in (1, 2):
+            for i in (2, 1):
                 nc.sync.dma_start(x_sb[i, c][:], x_dram[i][:, :, c * CHUNK : (c + 1) * CHUNK])
 
         identity = held.tile([P, P], BF16, name="identity")
@@ -204,42 +204,40 @@ def tile_dynamicmetaembedding_b_kernel(tc, table, w0, b0, x1, w1, b1, x2, w2, b2
             nc.vector.tensor_tensor(part[:], p_i, att[:, i, first : first + width].unsqueeze(1).to_broadcast(whole), ALU.mult)
             return part
 
-        p1_sb = held.tile([P, MB, N], BF16, name="p1_sb")
+        p2_sb = held.tile([P, MB, N], BF16, name="p2_sb")
         both = held.tile([P, MB, N], BF16, name="both")
         out_blocks = out.rearrange("(a p) j -> p a j", p=P)
 
-        def first_source(c):
-            project(1, c * CHUNK, CHUNK, p1_sb[:, :, c * CHUNK : (c + 1) * CHUNK])
+        def shorter_source(c):
+            project(2, c * CHUNK, CHUNK, p2_sb[:, :, c * CHUNK : (c + 1) * CHUNK])
 
         def two_sources(c):
             here = slice(c * CHUNK, (c + 1) * CHUNK)
             part0 = weighted(0, p0_sb[:, :, here], c * CHUNK, CHUNK)
-            part1 = weighted(1, p1_sb[:, :, here], c * CHUNK, CHUNK)
-            nc.vector.tensor_tensor(both[:, :, here], part0[:], part1[:], ALU.add)
+            part2 = weighted(2, p2_sb[:, :, here], c * CHUNK, CHUNK)
+            nc.vector.tensor_tensor(both[:, :, here], part0[:], part2[:], ALU.add)
 
-        def last_source(t):
+        def longer_source(t):
             first = t * BATCH
             for width in WIDTHS[t]:
-                p2_sb = proj.tile([P, MB, width], BF16, name="p2_sb")
-                project(2, first, width, p2_sb)
-                part2 = weighted(2, p2_sb[:], first, width)
+                p1_sb = proj.tile([P, MB, width], BF16, name="p1_sb")
+                project(1, first, width, p1_sb)
+                part1 = weighted(1, p1_sb[:], first, width)
                 mixed = proj.tile([P, MB, width], F32, name="mixed")
-                nc.vector.tensor_tensor(mixed[:], both[:, :, first : first + width], part2[:], ALU.add)
+                nc.vector.tensor_tensor(mixed[:], both[:, :, first : first + width], part1[:], ALU.add)
                 nc.sync.dma_start(out_blocks[:, :, first : first + width], mixed[:])
                 first += width
 
-        first_source(0)
+        shorter_source(0)
+        shorter_source(1)
         c_all = constants()
-        share = weigh(0, c_all)
-        first_source(1)
-        spread(0, share)
+        for t in range(N // BATCH):
+            spread(t, weigh(t, c_all))
         two_sources(0)
         two_sources(1)
-        share = weigh(1, c_all)
-        last_source(0)
-        spread(1, share)
-        first_source(2)
+        longer_source(0)
+        shorter_source(2)
+        shorter_source(3)
         two_sources(2)
-        first_source(3)
         two_sources(3)
-        last_source(1)
+        longer_source(1)

@@ -19,7 +19,7 @@ QUARTERS = P // QUARTER
 SPAN = 256
 BATCH = QUARTERS * SPAN
 SOURCES = (0, 1, 2)
-WIDTHS = ((256, 256, 256, 256), (256, 256, 256, 128, 128))
+WIDTHS = ((512, 512), (512, 256, 128, 128))
 assert all(sum(widths) == BATCH for widths in WIDTHS) and len(WIDTHS) * BATCH == N
 
 FLOPS = 2 * M * N * (D + E1 + E2) + 2 * 3 * M * N
@@ -29,7 +29,7 @@ def tile_dynamicmetaembedding_b_kernel(tc, table, w0, b0, x1, w1, b1, x2, w2, b2
     nc = tc.nc
     with ExitStack() as ctx:
         held = ctx.enter_context(tc.tile_pool(name="held", bufs=1))
-        proj = ctx.enter_context(tc.tile_pool(name="proj", bufs=4))
+        proj = ctx.enter_context(tc.tile_pool(name="proj", bufs=8))
         soft = ctx.enter_context(tc.tile_pool(name="soft", bufs=2))
         work = ctx.enter_context(tc.tile_pool(name="work", bufs=2))
         bank = ctx.enter_context(tc.psum_pool(name="bank", bufs=8))
@@ -119,19 +119,18 @@ def tile_dynamicmetaembedding_b_kernel(tc, table, w0, b0, x1, w1, b1, x2, w2, b2
             v_col[i] = held.tile([P, depth[i]], BF16, name="v%d_col" % i)
             nc.vector.tensor_copy(v_col[i][:], v_sum[:])
 
-        def project(i, first, width, dest):
+        def project(i, a, first, width, dest):
             c, inside = first // CHUNK, first % CHUNK
-            for a in range(MB):
-                acc = bank.tile([P, width], F32, name="acc")
-                for k in range(depth[i]):
-                    nc.tensor.matmul(
-                        acc[:],
-                        w_sb[i][:, k, a * P : (a + 1) * P],
-                        x_sb[i, c][:, k, inside : inside + width],
-                        start=(k == 0),
-                        stop=(k == depth[i] - 1),
-                    )
-                leave_bank("scalar", dest[:, a, :], acc, i, a)
+            acc = bank.tile([P, width], F32, name="acc")
+            for k in range(depth[i]):
+                nc.tensor.matmul(
+                    acc[:],
+                    w_sb[i][:, k, a * P : (a + 1) * P],
+                    x_sb[i, c][:, k, inside : inside + width],
+                    start=(k == 0),
+                    stop=(k == depth[i] - 1),
+                )
+            leave_bank("scalar", dest, acc, i, a)
 
         def constants():
             c_part = held.tile([P, len(SOURCES)], F32, name="c_part")
@@ -209,7 +208,8 @@ def tile_dynamicmetaembedding_b_kernel(tc, table, w0, b0, x1, w1, b1, x2, w2, b2
         out_blocks = out.rearrange("(a p) j -> p a j", p=P)
 
         def shorter_source(c):
-            project(2, c * CHUNK, CHUNK, p2_sb[:, :, c * CHUNK : (c + 1) * CHUNK])
+            for a in range(MB):
+                project(2, a, c * CHUNK, CHUNK, p2_sb[:, a, c * CHUNK : (c + 1) * CHUNK])
 
         def two_sources(c):
             here = slice(c * CHUNK, (c + 1) * CHUNK)
@@ -220,12 +220,15 @@ def tile_dynamicmetaembedding_b_kernel(tc, table, w0, b0, x1, w1, b1, x2, w2, b2
         def longer_source(t):
             first = t * BATCH
             for width in WIDTHS[t]:
-                p1_sb = proj.tile([P, MB, width], BF16, name="p1_sb")
-                project(1, first, width, p1_sb)
-                part1 = weighted(1, p1_sb[:], first, width)
-                mixed = proj.tile([P, MB, width], F32, name="mixed")
-                nc.vector.tensor_tensor(mixed[:], both[:, :, first : first + width], part1[:], ALU.add)
-                nc.sync.dma_start(out_blocks[:, :, first : first + width], mixed[:])
+                here = slice(first, first + width)
+                for a in range(MB):
+                    p1_sb = proj.tile([P, width], BF16, name="p1_sb")
+                    project(1, a, first, width, p1_sb[:])
+                    part1 = proj.tile([P, width], BF16, name="part1")
+                    nc.vector.tensor_tensor(part1[:], p1_sb[:], att[:, 1, here], ALU.mult)
+                    mixed = proj.tile([P, width], F32, name="mixed")
+                    nc.vector.tensor_tensor(mixed[:], both[:, a, here], part1[:], ALU.add)
+                    nc.sync.dma_start(out_blocks[:, a, here], mixed[:])
                 first += width
 
         shorter_source(0)

@@ -29,7 +29,8 @@ def tile_dynamicmetaembedding_b_kernel(tc, table, w0, b0, x1, w1, b1, x2, w2, b2
     nc = tc.nc
     with ExitStack() as ctx:
         held = ctx.enter_context(tc.tile_pool(name="held", bufs=1))
-        proj = ctx.enter_context(tc.tile_pool(name="proj", bufs=8))
+        proj = ctx.enter_context(tc.tile_pool(name="proj", bufs=12))
+        done = ctx.enter_context(tc.tile_pool(name="done", bufs=6))
         soft = ctx.enter_context(tc.tile_pool(name="soft", bufs=2))
         work = ctx.enter_context(tc.tile_pool(name="work", bufs=2))
         bank = ctx.enter_context(tc.psum_pool(name="bank", bufs=8))
@@ -37,7 +38,7 @@ def tile_dynamicmetaembedding_b_kernel(tc, table, w0, b0, x1, w1, b1, x2, w2, b2
         offsets = held.tile([P, N // 16], U16, name="offsets")
         words = held.tile([P, SB // TURNED, TURNED, D], BF16, name="words")
         w0_sb = held.tile([P, M], BF16, name="w0_sb")
-        depth = {0: MB, 1: E1 // P, 2: E2 // P}
+        depth = {0: 1, 1: E1 // P, 2: E2 // P}
         w_sb = {i: held.tile([P, depth[i], M], BF16, name="w%d_sb" % i) for i in (1, 2)}
         x_sb = {
             (i, c): held.tile([P, depth[i], CHUNK], BF16, name="x%d_%d" % (i, c))
@@ -108,7 +109,7 @@ def tile_dynamicmetaembedding_b_kernel(tc, table, w0, b0, x1, w1, b1, x2, w2, b2
                 nc.tensor.matmul(acc[:], w0_sb[:, a * P : (a + 1) * P], picked, start=True, stop=True)
                 leave_bank("scalar" if a % 2 == 0 else "vector", p0_sb[:, a, c * CHUNK : (c + 1) * CHUNK], acc, 0, a)
 
-        v_col = {0: wa_col}
+        v_col = {0: ones}
         for i in (1, 2):
             v_sum = held.tile([P, depth[i]], F32, name="v%d_sum" % i)
             for k in range(depth[i]):
@@ -118,6 +119,15 @@ def tile_dynamicmetaembedding_b_kernel(tc, table, w0, b0, x1, w1, b1, x2, w2, b2
                 )
             v_col[i] = held.tile([P, depth[i]], BF16, name="v%d_col" % i)
             nc.vector.tensor_copy(v_col[i][:], v_sum[:])
+
+        folded = held.tile([P, N], BF16, name="folded")
+        for t in range(N // BATCH):
+            batch = slice(t * BATCH, (t + 1) * BATCH)
+            nc.vector.tensor_scalar(folded[:, batch], p0_sb[:, 0, batch], wa_col[:, 0:1], None, ALU.mult)
+            for a in range(1, MB):
+                scaled = work.tile([P, BATCH], BF16, name="scaled")
+                nc.vector.tensor_scalar(scaled[:], p0_sb[:, a, batch], wa_col[:, a : a + 1], None, ALU.mult)
+                nc.vector.tensor_tensor(folded[:, batch], folded[:, batch], scaled[:], ALU.add)
 
         def project(i, a, first, width, dest):
             c, inside = first // CHUNK, first % CHUNK
@@ -150,14 +160,14 @@ def tile_dynamicmetaembedding_b_kernel(tc, table, w0, b0, x1, w1, b1, x2, w2, b2
 
         def summed_over(i, k, first, width):
             if i == 0:
-                return p0_sb[:, k, first : first + width]
+                return folded[:, first : first + width]
             c, inside = first // CHUNK, first % CHUNK
             return x_sb[i, c][:, k, inside : inside + width]
 
         def weigh(t, c_all):
             by_source = [P, len(SOURCES), SPAN]
             logit = soft.tile(by_source, F32, name="logit")
-            for i in SOURCES:
+            for i in (1, 2, 0):
                 rows = bank.tile([P, SPAN], F32, name="rows", tag="acc")
                 for k in range(depth[i]):
                     for q in range(QUARTERS):
@@ -224,9 +234,9 @@ def tile_dynamicmetaembedding_b_kernel(tc, table, w0, b0, x1, w1, b1, x2, w2, b2
                 for a in range(MB):
                     p1_sb = proj.tile([P, width], BF16, name="p1_sb")
                     project(1, a, first, width, p1_sb[:])
-                    part1 = proj.tile([P, width], BF16, name="part1")
+                    part1 = work.tile([P, width], BF16, name="part1")
                     nc.vector.tensor_tensor(part1[:], p1_sb[:], att[:, 1, here], ALU.mult)
-                    mixed = proj.tile([P, width], F32, name="mixed")
+                    mixed = done.tile([P, width], F32, name="mixed")
                     nc.vector.tensor_tensor(mixed[:], both[:, a, here], part1[:], ALU.add)
                     nc.sync.dma_start(out_blocks[:, a, here], mixed[:])
                 first += width

@@ -14,6 +14,7 @@ CHUNKS = N // CHUNK
 MB = M // P
 SB = S // P
 TURNED = 4
+GROUPS = SB // TURNED
 QUARTER = 32
 QUARTERS = P // QUARTER
 SPAN = 256
@@ -21,6 +22,7 @@ BATCH = QUARTERS * SPAN
 SOURCES = (0, 1, 2)
 WIDTHS = ((512, 512), (512, 256, 128, 128))
 assert all(sum(widths) == BATCH for widths in WIDTHS) and len(WIDTHS) * BATCH == N
+assert E1 // P == CHUNKS * MB // 2
 
 FLOPS = 2 * M * N * (D + E1 + E2) + 2 * 3 * M * N
 
@@ -57,16 +59,20 @@ def tile_dynamicmetaembedding_b_kernel(tc, table, w0, b0, x1, w1, b1, x2, w2, b2
                 nc.sync.dma_start(dest[:], vector.rearrange("(a p) o -> p (a o)", p=P))
 
         load_column(wa_col, wa)
-        for g in range(SB // TURNED):
+        for g in range(GROUPS):
             nc.sync.dma_start(words[:, g, :, :].rearrange("p r d -> p (r d)"), table_runs[:, g, :])
+            k = g - (GROUPS - depth[2])
+            if k >= 0:
+                nc.sync.dma_start(w_sb[2][:, k, :], w_dram[2][:, k, :])
+                nc.sync.dma_start(x_sb[2, 0][:, k, :], x_dram[2][:, k, 0:CHUNK])
         nc.sync.dma_start(offsets[:], offs)
         nc.sync.dma_start(w0_sb[:], w0)
-        load_column(bias[0], b0)
-        for i in (2, 1):
-            nc.sync.dma_start(w_sb[i][:], w_dram[i])
         load_column(bias[2], b2)
+        load_column(bias[0], b0)
+        nc.sync.dma_start(w_sb[1][:], w_dram[1])
         load_column(bias[1], b1)
-        for c in range(CHUNKS):
+        nc.sync.dma_start(x_sb[1, 0][:], x_dram[1][:, :, 0:CHUNK])
+        for c in range(1, CHUNKS):
             for i in (2, 1):
                 nc.sync.dma_start(x_sb[i, c][:], x_dram[i][:, :, c * CHUNK : (c + 1) * CHUNK])
 
@@ -89,8 +95,18 @@ def tile_dynamicmetaembedding_b_kernel(tc, table, w0, b0, x1, w1, b1, x2, w2, b2
         wa_row = held.tile([P, M], BF16, name="wa_row")
         nc.vector.tensor_copy(wa_row[:], wa_wide[:])
 
+        v_sum = {i: held.tile([P, depth[i]], F32, name="v%d_sum" % i) for i in (1, 2)}
+
+        def v_block(i, k):
+            product = work.tile([P, M], F32, name="product")
+            nc.vector.scalar_tensor_tensor(
+                product[:], w_sb[i][:, k, :], 1.0, wa_row[:], ALU.mult, ALU.mult, accum_out=v_sum[i][:, k : k + 1]
+            )
+
         window = held.tile([P, S], BF16, name="window")
-        for g in range(SB // TURNED):
+        p2_sb = held.tile([P, MB, N], BF16, name="p2_sb")
+        opened = [bank.tile([P, CHUNK], F32, name="opened%d" % a, tag="acc") for a in range(MB)]
+        for g in range(GROUPS):
             turned = bank.tile([P, TURNED * P], BF16, name="turned", tag="acc")
             for r in range(TURNED):
                 nc.tensor.transpose(turned[:, r * P : (r + 1) * P], words[:, g, r, :], identity[:])
@@ -100,6 +116,19 @@ def tile_dynamicmetaembedding_b_kernel(tc, table, w0, b0, x1, w1, b1, x2, w2, b2
                 nc.vector.tensor_copy(in_order, as_turned)
             else:
                 nc.scalar.copy(in_order, as_turned)
+            k = g - (GROUPS - depth[2])
+            if k >= 0:
+                v_block(2, k)
+                for a in range(MB):
+                    nc.tensor.matmul(
+                        opened[a][:],
+                        w_sb[2][:, k, a * P : (a + 1) * P],
+                        x_sb[2, 0][:, k, :],
+                        start=(k == 0),
+                        stop=(k == depth[2] - 1),
+                    )
+        for a in range(MB):
+            leave_bank("scalar" if a % 2 == 0 else "vector", p2_sb[:, a, 0:CHUNK], opened[a], 2, a)
 
         p0_sb = held.tile([P, MB, N], BF16, name="p0_sb")
         for c in range(CHUNKS):
@@ -108,17 +137,13 @@ def tile_dynamicmetaembedding_b_kernel(tc, table, w0, b0, x1, w1, b1, x2, w2, b2
                 acc = bank.tile([P, CHUNK], F32, name="acc")
                 nc.tensor.matmul(acc[:], w0_sb[:, a * P : (a + 1) * P], picked, start=True, stop=True)
                 leave_bank("scalar" if a % 2 == 0 else "vector", p0_sb[:, a, c * CHUNK : (c + 1) * CHUNK], acc, 0, a)
+                if a % 2 == 1:
+                    v_block(1, c * (MB // 2) + a // 2)
 
         v_col = {0: ones}
         for i in (1, 2):
-            v_sum = held.tile([P, depth[i]], F32, name="v%d_sum" % i)
-            for k in range(depth[i]):
-                product = work.tile([P, M], F32, name="product")
-                nc.vector.scalar_tensor_tensor(
-                    product[:], w_sb[i][:, k, :], 1.0, wa_row[:], ALU.mult, ALU.mult, accum_out=v_sum[:, k : k + 1]
-                )
             v_col[i] = held.tile([P, depth[i]], BF16, name="v%d_col" % i)
-            nc.vector.tensor_copy(v_col[i][:], v_sum[:])
+            nc.vector.tensor_copy(v_col[i][:], v_sum[i][:])
 
         folded = held.tile([P, N], BF16, name="folded")
         for t in range(N // BATCH):
@@ -213,7 +238,6 @@ def tile_dynamicmetaembedding_b_kernel(tc, table, w0, b0, x1, w1, b1, x2, w2, b2
             nc.vector.tensor_tensor(part[:], p_i, att[:, i, first : first + width].unsqueeze(1).to_broadcast(whole), ALU.mult)
             return part
 
-        p2_sb = held.tile([P, MB, N], BF16, name="p2_sb")
         both = held.tile([P, MB, N], BF16, name="both")
         out_blocks = out.rearrange("(a p) j -> p a j", p=P)
 
@@ -241,7 +265,6 @@ def tile_dynamicmetaembedding_b_kernel(tc, table, w0, b0, x1, w1, b1, x2, w2, b2
                     nc.sync.dma_start(out_blocks[:, a, here], mixed[:])
                 first += width
 
-        shorter_source(0)
         shorter_source(1)
         c_all = constants()
         for t in range(N // BATCH):

@@ -43,9 +43,9 @@ def tile_dynamicmetaembedding_b_kernel(tc, table, w0, b0, x1, w1, b1, x2, w2, b2
         depth = {0: 1, 1: E1 // P, 2: E2 // P}
         w_sb = {i: held.tile([P, depth[i], M], BF16, name="w%d_sb" % i) for i in (1, 2)}
         x_sb = {
-            (i, c): held.tile([P, depth[i], CHUNK], BF16, name="x%d_%d" % (i, c))
+            (i, t): held.tile([P, depth[i], BATCH], BF16, name="x%d_%d" % (i, t))
             for i in (1, 2)
-            for c in range(CHUNKS)
+            for t in range(N // BATCH)
         }
         bias = {i: held.tile([P, MB], F32, name="bias%d" % i) for i in SOURCES}
         wa_col = held.tile([P, MB], BF16, name="wa_col")
@@ -64,17 +64,17 @@ def tile_dynamicmetaembedding_b_kernel(tc, table, w0, b0, x1, w1, b1, x2, w2, b2
             k = g - (GROUPS - depth[2])
             if k >= 0:
                 nc.sync.dma_start(w_sb[2][:, k, :], w_dram[2][:, k, :])
-                nc.sync.dma_start(x_sb[2, 0][:, k, :], x_dram[2][:, k, 0:CHUNK])
+                nc.sync.dma_start(x_sb[2, 0][:, k, 0:CHUNK], x_dram[2][:, k, 0:CHUNK])
         nc.sync.dma_start(offsets[:], offs)
         nc.sync.dma_start(w0_sb[:], w0)
         load_column(bias[2], b2)
         load_column(bias[0], b0)
+        nc.sync.dma_start(x_sb[2, 0][:, :, CHUNK:BATCH], x_dram[2][:, :, CHUNK:BATCH])
         nc.sync.dma_start(w_sb[1][:], w_dram[1])
         load_column(bias[1], b1)
-        nc.sync.dma_start(x_sb[1, 0][:], x_dram[1][:, :, 0:CHUNK])
-        for c in range(1, CHUNKS):
-            for i in (2, 1):
-                nc.sync.dma_start(x_sb[i, c][:], x_dram[i][:, :, c * CHUNK : (c + 1) * CHUNK])
+        nc.sync.dma_start(x_sb[1, 0][:], x_dram[1][:, :, 0:BATCH])
+        for i in (2, 1):
+            nc.sync.dma_start(x_sb[i, 1][:], x_dram[i][:, :, BATCH:N])
 
         identity = held.tile([P, P], BF16, name="identity")
         make_identity(nc, identity[:])
@@ -123,7 +123,7 @@ def tile_dynamicmetaembedding_b_kernel(tc, table, w0, b0, x1, w1, b1, x2, w2, b2
                     nc.tensor.matmul(
                         opened[a][:],
                         w_sb[2][:, k, a * P : (a + 1) * P],
-                        x_sb[2, 0][:, k, :],
+                        x_sb[2, 0][:, k, 0:CHUNK],
                         start=(k == 0),
                         stop=(k == depth[2] - 1),
                     )
@@ -155,13 +155,13 @@ def tile_dynamicmetaembedding_b_kernel(tc, table, w0, b0, x1, w1, b1, x2, w2, b2
                 nc.vector.tensor_tensor(folded[:, batch], folded[:, batch], scaled[:], ALU.add)
 
         def project(i, a, first, width, dest):
-            c, inside = first // CHUNK, first % CHUNK
+            t, inside = first // BATCH, first % BATCH
             acc = bank.tile([P, width], F32, name="acc")
             for k in range(depth[i]):
                 nc.tensor.matmul(
                     acc[:],
                     w_sb[i][:, k, a * P : (a + 1) * P],
-                    x_sb[i, c][:, k, inside : inside + width],
+                    x_sb[i, t][:, k, inside : inside + width],
                     start=(k == 0),
                     stop=(k == depth[i] - 1),
                 )
@@ -186,8 +186,8 @@ def tile_dynamicmetaembedding_b_kernel(tc, table, w0, b0, x1, w1, b1, x2, w2, b2
         def summed_over(i, k, first, width):
             if i == 0:
                 return folded[:, first : first + width]
-            c, inside = first // CHUNK, first % CHUNK
-            return x_sb[i, c][:, k, inside : inside + width]
+            t, inside = first // BATCH, first % BATCH
+            return x_sb[i, t][:, k, inside : inside + width]
 
         def weigh(t, c_all):
             by_source = [P, len(SOURCES), SPAN]

@@ -140,6 +140,16 @@ def tile_dynamicmetaembedding_b_kernel(tc, table, w0, b0, x1, w1, b1, x2, w2, b2
                 if a % 2 == 1:
                     v_block(1, c * (MB // 2) + a // 2)
 
+        c_part = held.tile([P, len(SOURCES)], F32, name="c_part")
+        nc.vector.memset(c_part[:], 0.0)
+        for i in (1, 2):
+            small = work.tile([P, MB], F32, name="small")
+            nc.vector.scalar_tensor_tensor(
+                small[:], bias[i][:], 1.0, wa_col[:], ALU.mult, ALU.mult, accum_out=c_part[:, i : i + 1]
+            )
+        c_round = held.tile([P, len(SOURCES)], BF16, name="c_round")
+        nc.vector.tensor_copy(c_round[:], c_part[:])
+
         v_col = {0: ones}
         for i in (1, 2):
             v_col[i] = held.tile([P, depth[i]], BF16, name="v%d_col" % i)
@@ -167,20 +177,11 @@ def tile_dynamicmetaembedding_b_kernel(tc, table, w0, b0, x1, w1, b1, x2, w2, b2
                 )
             leave_bank("scalar", dest, acc, i, a)
 
-        def constants():
-            c_part = held.tile([P, len(SOURCES)], F32, name="c_part")
-            nc.vector.memset(c_part[:], 0.0)
-            for i in (1, 2):
-                small = work.tile([P, MB], F32, name="small")
-                nc.vector.scalar_tensor_tensor(
-                    small[:], bias[i][:], 1.0, wa_col[:], ALU.mult, ALU.mult, accum_out=c_part[:, i : i + 1]
-                )
-            c_round = held.tile([P, len(SOURCES)], BF16, name="c_round")
-            nc.vector.tensor_copy(c_round[:], c_part[:])
+        def constants(c_round):
             c_bank = bank.tile([P, len(SOURCES)], F32, name="c_bank", tag="acc")
             nc.tensor.matmul(c_bank[:], ones[:], c_round[:], start=True, stop=True)
             c_all = held.tile([P, len(SOURCES)], F32, name="c_all")
-            nc.vector.tensor_copy(c_all[:], c_bank[:])
+            nc.scalar.copy(c_all[:], c_bank[:])
             return c_all
 
         def summed_over(i, k, first, width):
@@ -266,7 +267,7 @@ def tile_dynamicmetaembedding_b_kernel(tc, table, w0, b0, x1, w1, b1, x2, w2, b2
                 first += width
 
         shorter_source(1)
-        c_all = constants()
+        c_all = constants(c_round)
         for t in range(N // BATCH):
             spread(t, weigh(t, c_all))
         two_sources(0)

@@ -40,7 +40,7 @@ def tile_dynamicmetaembedding_b_kernel(tc, table, w0, b0, x1, w1, b1, x2, w2, b2
         offsets = held.tile([P, N // 16], U16, name="offsets")
         words = held.tile([P, SB // TURNED, TURNED, D], BF16, name="words")
         w0_sb = held.tile([P, M], BF16, name="w0_sb")
-        depth = {0: 1, 1: E1 // P, 2: E2 // P}
+        depth = {0: MB, 1: E1 // P, 2: E2 // P}
         w_sb = {i: held.tile([P, depth[i], M], BF16, name="w%d_sb" % i) for i in (1, 2)}
         x_sb = {
             (i, t): held.tile([P, depth[i], BATCH], BF16, name="x%d_%d" % (i, t))
@@ -67,11 +67,10 @@ def tile_dynamicmetaembedding_b_kernel(tc, table, w0, b0, x1, w1, b1, x2, w2, b2
                 nc.sync.dma_start(x_sb[2, 0][:, k, 0:CHUNK], x_dram[2][:, k, 0:CHUNK])
         nc.sync.dma_start(offsets[:], offs)
         nc.sync.dma_start(w0_sb[:], w0)
-        load_column(bias[2], b2)
-        load_column(bias[0], b0)
-        nc.sync.dma_start(x_sb[2, 0][:, :, CHUNK:BATCH], x_dram[2][:, :, CHUNK:BATCH])
+        for i, b_i in ((2, b2), (0, b0), (1, b1)):
+            load_column(bias[i], b_i)
         nc.sync.dma_start(w_sb[1][:], w_dram[1])
-        load_column(bias[1], b1)
+        nc.sync.dma_start(x_sb[2, 0][:, :, CHUNK:BATCH], x_dram[2][:, :, CHUNK:BATCH])
         nc.sync.dma_start(x_sb[1, 0][:], x_dram[1][:, :, 0:BATCH])
         for i in (2, 1):
             nc.sync.dma_start(x_sb[i, 1][:], x_dram[i][:, :, BATCH:N])
@@ -130,16 +129,6 @@ def tile_dynamicmetaembedding_b_kernel(tc, table, w0, b0, x1, w1, b1, x2, w2, b2
         for a in range(MB):
             leave_bank("scalar" if a % 2 == 0 else "vector", p2_sb[:, a, 0:CHUNK], opened[a], 2, a)
 
-        p0_sb = held.tile([P, MB, N], BF16, name="p0_sb")
-        for c in range(CHUNKS):
-            picked = window[:].indirect(offsets[:, c * (CHUNK // 16) : (c + 1) * (CHUNK // 16)])
-            for a in range(MB):
-                acc = bank.tile([P, CHUNK], F32, name="acc")
-                nc.tensor.matmul(acc[:], w0_sb[:, a * P : (a + 1) * P], picked, start=True, stop=True)
-                leave_bank("scalar" if a % 2 == 0 else "vector", p0_sb[:, a, c * CHUNK : (c + 1) * CHUNK], acc, 0, a)
-                if a % 2 == 1:
-                    v_block(1, c * (MB // 2) + a // 2)
-
         c_part = held.tile([P, len(SOURCES)], F32, name="c_part")
         nc.vector.memset(c_part[:], 0.0)
         for i in (1, 2):
@@ -150,19 +139,21 @@ def tile_dynamicmetaembedding_b_kernel(tc, table, w0, b0, x1, w1, b1, x2, w2, b2
         c_round = held.tile([P, len(SOURCES)], BF16, name="c_round")
         nc.vector.tensor_copy(c_round[:], c_part[:])
 
-        v_col = {0: ones}
+        v_col = {0: wa_col}
         for i in (1, 2):
             v_col[i] = held.tile([P, depth[i]], BF16, name="v%d_col" % i)
-            nc.vector.tensor_copy(v_col[i][:], v_sum[i][:])
+        nc.vector.tensor_copy(v_col[2][:], v_sum[2][:])
 
-        folded = held.tile([P, N], BF16, name="folded")
-        for t in range(N // BATCH):
-            batch = slice(t * BATCH, (t + 1) * BATCH)
-            nc.vector.tensor_scalar(folded[:, batch], p0_sb[:, 0, batch], wa_col[:, 0:1], None, ALU.mult)
-            for a in range(1, MB):
-                scaled = work.tile([P, BATCH], BF16, name="scaled")
-                nc.vector.tensor_scalar(scaled[:], p0_sb[:, a, batch], wa_col[:, a : a + 1], None, ALU.mult)
-                nc.vector.tensor_tensor(folded[:, batch], folded[:, batch], scaled[:], ALU.add)
+        p0_sb = held.tile([P, MB, N], BF16, name="p0_sb")
+        for c in range(CHUNKS):
+            picked = window[:].indirect(offsets[:, c * (CHUNK // 16) : (c + 1) * (CHUNK // 16)])
+            for a in range(MB):
+                acc = bank.tile([P, CHUNK], F32, name="acc")
+                nc.tensor.matmul(acc[:], w0_sb[:, a * P : (a + 1) * P], picked, start=True, stop=True)
+                if a < MB // 2:
+                    v_block(1, c * (MB // 2) + a)
+                leave_bank("vector" if a == MB - 1 else "scalar", p0_sb[:, a, c * CHUNK : (c + 1) * CHUNK], acc, 0, a)
+        nc.vector.tensor_copy(v_col[1][:], v_sum[1][:])
 
         def project(i, a, first, width, dest):
             t, inside = first // BATCH, first % BATCH
@@ -186,14 +177,14 @@ def tile_dynamicmetaembedding_b_kernel(tc, table, w0, b0, x1, w1, b1, x2, w2, b2
 
         def summed_over(i, k, first, width):
             if i == 0:
-                return folded[:, first : first + width]
+                return p0_sb[:, k, first : first + width]
             t, inside = first // BATCH, first % BATCH
             return x_sb[i, t][:, k, inside : inside + width]
 
         def weigh(t, c_all):
             by_source = [P, len(SOURCES), SPAN]
             logit = soft.tile(by_source, F32, name="logit")
-            for i in (1, 2, 0):
+            for i in (2, 0, 1):
                 rows = bank.tile([P, SPAN], F32, name="rows", tag="acc")
                 for k in range(depth[i]):
                     for q in range(QUARTERS):
@@ -266,10 +257,10 @@ def tile_dynamicmetaembedding_b_kernel(tc, table, w0, b0, x1, w1, b1, x2, w2, b2
                     nc.sync.dma_start(out_blocks[:, a, here], mixed[:])
                 first += width
 
-        shorter_source(1)
         c_all = constants(c_round)
-        for t in range(N // BATCH):
-            spread(t, weigh(t, c_all))
+        spread(0, weigh(0, c_all))
+        shorter_source(1)
+        spread(1, weigh(1, c_all))
         two_sources(0)
         two_sources(1)
         longer_source(0)

@@ -214,15 +214,15 @@ def tile_dynamicmetaembedding_b_kernel(tc, table, w0, b0, x1, w1, b1, x2, w2, b2
 
         att = held.tile([P, len(SOURCES), N], BF16, name="att")
 
-        parked = out[0 : len(SOURCES), N - BATCH : N].bitcast(BF16)
+        parked = out[0 : QUARTER * len(SOURCES), N - BATCH : N].bitcast(BF16).rearrange("(r i) j -> r i j", i=len(SOURCES))
 
         def spread(t, share):
             for q in range(QUARTERS):
                 first = t * BATCH + q * SPAN
-                nc.sync.dma_start(parked[:, first : first + SPAN].unsqueeze(0), share[q * QUARTER : q * QUARTER + 1, :, :])
-            for i in SOURCES:
-                batch = slice(t * BATCH, (t + 1) * BATCH)
-                nc.sync.dma_start(att[:, i, batch], parked[i, batch].partition_broadcast(P))
+                nc.sync.dma_start(parked[:, :, first : first + SPAN], share[q * QUARTER : (q + 1) * QUARTER, :, :])
+            batch = slice(t * BATCH, (t + 1) * BATCH)
+            for q in range(QUARTERS):
+                nc.sync.dma_start(att[q * QUARTER : (q + 1) * QUARTER, :, batch], parked[:, :, batch])
 
         def weighted(i, p_i, first, width):
             whole = [P, MB, width]

@@ -257,10 +257,10 @@ def tile_dynamicmetaembedding_b_kernel(tc, table, w0, b0, x1, w1, b1, x2, w2, b2
                     nc.sync.dma_start(out_blocks[:, a, here], mixed[:])
                 first += width
 
-        c_all = constants(c_round)
-        spread(0, weigh(0, c_all))
         shorter_source(1)
-        spread(1, weigh(1, c_all))
+        c_all = constants(c_round)
+        for t in range(N // BATCH):
+            spread(t, weigh(t, c_all))
         two_sources(0)
         two_sources(1)
         longer_source(0)

@@ -20,8 +20,9 @@ QUARTERS = P // QUARTER
 SPAN = 256
 BATCH = QUARTERS * SPAN
 SOURCES = (0, 1, 2)
-WIDTHS = ((512, 512), (512, 256, 128, 128))
-assert all(sum(widths) == BATCH for widths in WIDTHS) and len(WIDTHS) * BATCH == N
+WIDTHS = ((512, 512), (512, 256, 128))
+LAST = 128
+assert sum(WIDTHS[0]) == BATCH and sum(WIDTHS[1]) + LAST == BATCH and len(WIDTHS) * BATCH == N
 assert E1 // P == CHUNKS * MB // 2
 
 FLOPS = 2 * M * N * (D + E1 + E2) + 2 * 3 * M * N
@@ -40,7 +41,7 @@ def tile_dynamicmetaembedding_b_kernel(tc, table, w0, b0, x1, w1, b1, x2, w2, b2
         offsets = held.tile([P, N // 16], U16, name="offsets")
         words = held.tile([P, SB // TURNED, TURNED, D], BF16, name="words")
         w0_sb = held.tile([P, M], BF16, name="w0_sb")
-        depth = {0: MB, 1: E1 // P, 2: E2 // P}
+        depth = {1: E1 // P, 2: E2 // P}
         w_sb = {i: held.tile([P, depth[i], M], BF16, name="w%d_sb" % i) for i in (1, 2)}
         x_sb = {
             (i, t): held.tile([P, depth[i], BATCH], BF16, name="x%d_%d" % (i, t))
@@ -139,9 +140,7 @@ def tile_dynamicmetaembedding_b_kernel(tc, table, w0, b0, x1, w1, b1, x2, w2, b2
         c_round = held.tile([P, len(SOURCES)], BF16, name="c_round")
         nc.vector.tensor_copy(c_round[:], c_part[:])
 
-        v_col = {0: wa_col}
-        for i in (1, 2):
-            v_col[i] = held.tile([P, depth[i]], BF16, name="v%d_col" % i)
+        v_col = {i: held.tile([P, depth[i]], BF16, name="v%d_col" % i) for i in (1, 2)}
         nc.vector.tensor_copy(v_col[2][:], v_sum[2][:])
 
         p0_sb = held.tile([P, MB, N], BF16, name="p0_sb")
@@ -175,25 +174,36 @@ def tile_dynamicmetaembedding_b_kernel(tc, table, w0, b0, x1, w1, b1, x2, w2, b2
             nc.scalar.copy(c_all[:], c_bank[:])
             return c_all
 
-        def summed_over(i, k, first, width):
+        late = slice(N - BATCH, N)
+        folded = held.tile([P, BATCH], BF16, name="folded")
+        nc.vector.tensor_scalar(folded[:], p0_sb[:, 0, late], wa_col[:, 0:1], None, ALU.mult)
+        for a in range(1, MB):
+            scaled = work.tile([P, BATCH], BF16, name="scaled")
+            nc.vector.tensor_scalar(scaled[:], p0_sb[:, a, late], wa_col[:, a : a + 1], None, ALU.mult)
+            nc.vector.tensor_tensor(folded[:], folded[:], scaled[:], ALU.add)
+
+        def summands(i, t):
+            batch = slice(t * BATCH, (t + 1) * BATCH)
+            if i == 0 and t == 1:
+                return [(ones[:, 0:1], folded[:])]
             if i == 0:
-                return p0_sb[:, k, first : first + width]
-            t, inside = first // BATCH, first % BATCH
-            return x_sb[i, t][:, k, inside : inside + width]
+                return [(wa_col[:, a : a + 1], p0_sb[:, a, batch]) for a in range(MB)]
+            return [(v_col[i][:, k : k + 1], x_sb[i, t][:, k, :]) for k in range(depth[i])]
 
         def weigh(t, c_all):
             by_source = [P, len(SOURCES), SPAN]
             logit = soft.tile(by_source, F32, name="logit")
             for i in (2, 0, 1):
                 rows = bank.tile([P, SPAN], F32, name="rows", tag="acc")
-                for k in range(depth[i]):
+                pairs = summands(i, t)
+                for k, (weights, block) in enumerate(pairs):
                     for q in range(QUARTERS):
                         nc.tensor.matmul(
                             rows[q * QUARTER : (q + 1) * QUARTER, :],
-                            v_col[i][:, k : k + 1].to_broadcast([P, QUARTER]),
-                            summed_over(i, k, t * BATCH + q * SPAN, SPAN),
+                            weights.to_broadcast([P, QUARTER]),
+                            block[:, q * SPAN : (q + 1) * SPAN],
                             start=(k == 0),
-                            stop=(k == depth[i] - 1),
+                            stop=(k == len(pairs) - 1),
                         )
                 nc.scalar.activation(logit[:, i, :], rows[:], ACT.Identity, bias=c_all[:, i : i + 1])
             top = soft.tile([P, SPAN], F32, name="top")
@@ -257,6 +267,25 @@ def tile_dynamicmetaembedding_b_kernel(tc, table, w0, b0, x1, w1, b1, x2, w2, b2
                     nc.sync.dma_start(out_blocks[:, a, here], mixed[:])
                 first += width
 
+        def last_piece():
+            here = slice(N - LAST, N)
+            deep = [P, depth[1], LAST]
+            weighed = work.tile(deep, BF16, name="weighed")
+            a_1 = att[:, 1, here]
+            nc.vector.tensor_tensor(weighed[:], x_sb[1, 1][:, :, BATCH - LAST : BATCH], a_1.unsqueeze(1).to_broadcast(deep), ALU.mult)
+            rest = work.tile([P, MB, LAST], F32, name="rest")
+            for a in range(MB):
+                nc.vector.scalar_tensor_tensor(rest[:, a, :], a_1, bias[1][:, a : a + 1], both[:, a, here], ALU.mult, ALU.add)
+            for a in range(MB):
+                acc = bank.tile([P, LAST], F32, name="acc")
+                for k in range(depth[1]):
+                    nc.tensor.matmul(
+                        acc[:], w_sb[1][:, k, a * P : (a + 1) * P], weighed[:, k, :], start=(k == 0), stop=(k == depth[1] - 1)
+                    )
+                mixed = done.tile([P, LAST], F32, name="mixed")
+                nc.vector.tensor_tensor(mixed[:], acc[:], rest[:, a, :], ALU.add)
+                nc.sync.dma_start(out_blocks[:, a, here], mixed[:])
+
         shorter_source(1)
         c_all = constants(c_round)
         for t in range(N // BATCH):
@@ -269,3 +298,4 @@ def tile_dynamicmetaembedding_b_kernel(tc, table, w0, b0, x1, w1, b1, x2, w2, b2
         two_sources(2)
         two_sources(3)
         longer_source(1)
+        last_piece()

from contextlib import ExitStack

import concourse.mybir as mybir
from concourse.masks import make_identity

BF16, F32, U16 = mybir.dt.bfloat16, mybir.dt.float32, mybir.dt.uint16
ACT = mybir.ActivationFunctionType
ALU = mybir.AluOpType

P = 128
S, D, M, N, E1, E2 = 4096, 128, 512, 2048, 1024, 768
CHUNK = 512
CHUNKS = N // CHUNK
MB = M // P
SB = S // P
TURNED = 4
GROUPS = SB // TURNED
QUARTER = 32
QUARTERS = P // QUARTER
SPAN = 256
BATCH = QUARTERS * SPAN
SOURCES = (0, 1, 2)
WIDTHS = ((512, 512), (512, 256, 128))
LAST = 128
assert sum(WIDTHS[0]) == BATCH and sum(WIDTHS[1]) + LAST == BATCH and len(WIDTHS) * BATCH == N
assert E1 // P == CHUNKS * MB // 2

FLOPS = 2 * M * N * (D + E1 + E2) + 2 * 3 * M * N


def tile_dynamicmetaembedding_b_kernel(tc, table, w0, b0, x1, w1, b1, x2, w2, b2, wa, offs, out):
    nc = tc.nc
    with ExitStack() as ctx:
        held = ctx.enter_context(tc.tile_pool(name="held", bufs=1))
        proj = ctx.enter_context(tc.tile_pool(name="proj", bufs=12))
        done = ctx.enter_context(tc.tile_pool(name="done", bufs=6))
        soft = ctx.enter_context(tc.tile_pool(name="soft", bufs=2))
        work = ctx.enter_context(tc.tile_pool(name="work", bufs=2))
        bank = ctx.enter_context(tc.psum_pool(name="bank", bufs=8))

        offsets = held.tile([P, N // 16], U16, name="offsets")
        words = held.tile([P, SB // TURNED, TURNED, D], BF16, name="words")
        w0_sb = held.tile([P, M], BF16, name="w0_sb")
        depth = {1: E1 // P, 2: E2 // P}
        w_sb = {i: held.tile([P, depth[i], M], BF16, name="w%d_sb" % i) for i in (1, 2)}
        x_sb = {
            (i, t): held.tile([P, depth[i], BATCH], BF16, name="x%d_%d" % (i, t))
            for i in (1, 2)
            for t in range(N // BATCH)
        }
        bias = {i: held.tile([P, MB], F32, name="bias%d" % i) for i in SOURCES}
        wa_col = held.tile([P, MB], BF16, name="wa_col")

        table_runs = table.rearrange("(g p r) d -> p g (r d)", p=P, r=TURNED)
        x_dram = {1: x1.rearrange("(k p) j -> p k j", p=P), 2: x2.rearrange("(k p) j -> p k j", p=P)}
        w_dram = {1: w1.rearrange("(k p) m -> p k m", p=P), 2: w2.rearrange("(k p) m -> p k m", p=P)}

        def load_column(dest, vector):
            with nc.allow_non_contiguous_dma(reason="one value to a partition: 512 small pieces, once"):
                nc.sync.dma_start(dest[:], vector.rearrange("(a p) o -> p (a o)", p=P))

        load_column(wa_col, wa)
        for g in range(GROUPS):
            nc.sync.dma_start(words[:, g, :, :].rearrange("p r d -> p (r d)"), table_runs[:, g, :])
            k = g - (GROUPS - depth[2])
            if k >= 0:
                nc.sync.dma_start(w_sb[2][:, k, :], w_dram[2][:, k, :])
                nc.sync.dma_start(x_sb[2, 0][:, k, 0:CHUNK], x_dram[2][:, k, 0:CHUNK])
        nc.sync.dma_start(offsets[:], offs)
        nc.sync.dma_start(w0_sb[:], w0)
        for i, b_i in ((2, b2), (0, b0), (1, b1)):
            load_column(bias[i], b_i)
        nc.sync.dma_start(w_sb[1][:], w_dram[1])
        nc.sync.dma_start(x_sb[2, 0][:, :, CHUNK:BATCH], x_dram[2][:, :, CHUNK:BATCH])
        nc.sync.dma_start(x_sb[1, 0][:], x_dram[1][:, :, 0:BATCH])
        for i in (2, 1):
            nc.sync.dma_start(x_sb[i, 1][:], x_dram[i][:, :, BATCH:N])

        identity = held.tile([P, P], BF16, name="identity")
        make_identity(nc, identity[:])
        ones = held.tile([P, P], BF16, name="ones")
        nc.vector.memset(ones[:], 1.0)

        def leave_bank(engine, dest, acc, i, a):
            if engine == "scalar":
                nc.scalar.activation(dest, acc[:], ACT.Identity, bias=bias[i][:, a : a + 1])
            else:
                nc.vector.tensor_scalar(dest, acc[:], bias[i][:, a : a + 1], None, ALU.add)

        wa_wide = bank.tile([P, M], F32, name="wa_wide", tag="acc")
        for a in range(MB):
            nc.tensor.matmul(
                wa_wide[:, a * P : (a + 1) * P], wa_col[:, a : a + 1].to_broadcast([P, P]), identity[:], start=True, stop=True
            )
        wa_row = held.tile([P, M], BF16, name="wa_row")
        nc.vector.tensor_copy(wa_row[:], wa_wide[:])

        v_sum = {i: held.tile([P, depth[i]], F32, name="v%d_sum" % i) for i in (1, 2)}

        def v_block(i, k):
            product = work.tile([P, M], F32, name="product")
            nc.vector.scalar_tensor_tensor(
                product[:], w_sb[i][:, k, :], 1.0, wa_row[:], ALU.mult, ALU.mult, accum_out=v_sum[i][:, k : k + 1]
            )

        window = held.tile([P, S], BF16, name="window")
        p2_sb = held.tile([P, MB, N], BF16, name="p2_sb")
        opened = [bank.tile([P, CHUNK], F32, name="opened%d" % a, tag="acc") for a in range(MB)]
        for g in range(GROUPS):
            turned = bank.tile([P, TURNED * P], BF16, name="turned", tag="acc")
            for r in range(TURNED):
                nc.tensor.transpose(turned[:, r * P : (r + 1) * P], words[:, g, r, :], identity[:])
            in_order = window[:, g * TURNED * P : (g + 1) * TURNED * P].rearrange("d (p r) -> d p r", r=TURNED)
            as_turned = turned[:].rearrange("d (r p) -> d p r", r=TURNED)
            if g % 2 == 0:
                nc.vector.tensor_copy(in_order, as_turned)
            else:
                nc.scalar.copy(in_order, as_turned)
            k = g - (GROUPS - depth[2])
            if k >= 0:
                v_block(2, k)
                for a in range(MB):
                    nc.tensor.matmul(
                        opened[a][:],
                        w_sb[2][:, k, a * P : (a + 1) * P],
                        x_sb[2, 0][:, k, 0:CHUNK],
                        start=(k == 0),
                        stop=(k == depth[2] - 1),
                    )
        for a in range(MB):
            leave_bank("scalar" if a % 2 == 0 else "vector", p2_sb[:, a, 0:CHUNK], opened[a], 2, a)

        c_part = held.tile([P, len(SOURCES)], F32, name="c_part")
        nc.vector.memset(c_part[:], 0.0)
        for i in (1, 2):
            small = work.tile([P, MB], F32, name="small")
            nc.vector.scalar_tensor_tensor(
                small[:], bias[i][:], 1.0, wa_col[:], ALU.mult, ALU.mult, accum_out=c_part[:, i : i + 1]
            )
        c_round = held.tile([P, len(SOURCES)], BF16, name="c_round")
        nc.vector.tensor_copy(c_round[:], c_part[:])

        v_col = {i: held.tile([P, depth[i]], BF16, name="v%d_col" % i) for i in (1, 2)}
        nc.vector.tensor_copy(v_col[2][:], v_sum[2][:])

        p0_sb = held.tile([P, MB, N], BF16, name="p0_sb")
        for c in range(CHUNKS):
            picked = window[:].indirect(offsets[:, c * (CHUNK // 16) : (c + 1) * (CHUNK // 16)])
            for a in range(MB):
                acc = bank.tile([P, CHUNK], F32, name="acc")
                nc.tensor.matmul(acc[:], w0_sb[:, a * P : (a + 1) * P], picked, start=True, stop=True)
                if a < MB // 2:
                    v_block(1, c * (MB // 2) + a)
                leave_bank("vector" if a == MB - 1 else "scalar", p0_sb[:, a, c * CHUNK : (c + 1) * CHUNK], acc, 0, a)
        nc.vector.tensor_copy(v_col[1][:], v_sum[1][:])

        def project(i, a, first, width, dest):
            t, inside = first // BATCH, first % BATCH
            acc = bank.tile([P, width], F32, name="acc")
            for k in range(depth[i]):
                nc.tensor.matmul(
                    acc[:],
                    w_sb[i][:, k, a * P : (a + 1) * P],
                    x_sb[i, t][:, k, inside : inside + width],
                    start=(k == 0),
                    stop=(k == depth[i] - 1),
                )
            leave_bank("scalar", dest, acc, i, a)

        def constants(c_round):
            c_bank = bank.tile([P, len(SOURCES)], F32, name="c_bank", tag="acc")
            nc.tensor.matmul(c_bank[:], ones[:], c_round[:], start=True, stop=True)
            c_all = held.tile([P, len(SOURCES)], F32, name="c_all")
            nc.scalar.copy(c_all[:], c_bank[:])
            return c_all

        late = slice(N - BATCH, N)
        folded = held.tile([P, BATCH], BF16, name="folded")
        nc.vector.tensor_scalar(folded[:], p0_sb[:, 0, late], wa_col[:, 0:1], None, ALU.mult)
        for a in range(1, MB):
            scaled = work.tile([P, BATCH], BF16, name="scaled")
            nc.vector.tensor_scalar(scaled[:], p0_sb[:, a, late], wa_col[:, a : a + 1], None, ALU.mult)
            nc.vector.tensor_tensor(folded[:], folded[:], scaled[:], ALU.add)

        def summands(i, t):
            batch = slice(t * BATCH, (t + 1) * BATCH)
            if i == 0 and t == 1:
                return [(ones[:, 0:1], folded[:])]
            if i == 0:
                return [(wa_col[:, a : a + 1], p0_sb[:, a, batch]) for a in range(MB)]
            return [(v_col[i][:, k : k + 1], x_sb[i, t][:, k, :]) for k in range(depth[i])]

        def weigh(t, c_all):
            by_source = [P, len(SOURCES), SPAN]
            logit = soft.tile(by_source, F32, name="logit")
            for i in (2, 0, 1):
                rows = bank.tile([P, SPAN], F32, name="rows", tag="acc")
                pairs = summands(i, t)
                for k, (weights, block) in enumerate(pairs):
                    for q in range(QUARTERS):
                        nc.tensor.matmul(
                            rows[q * QUARTER : (q + 1) * QUARTER, :],
                            weights.to_broadcast([P, QUARTER]),
                            block[:, q * SPAN : (q + 1) * SPAN],
                            start=(k == 0),
                            stop=(k == len(pairs) - 1),
                        )
                nc.scalar.activation(logit[:, i, :], rows[:], ACT.Identity, bias=c_all[:, i : i + 1])
            top = soft.tile([P, SPAN], F32, name="top")
            nc.vector.tensor_tensor(top[:], logit[:, 0, :], logit[:, 1, :], ALU.max)
            nc.vector.tensor_tensor(top[:], top[:], logit[:, 2, :], ALU.max)
            below = soft.tile(by_source, F32, name="below")
            nc.vector.tensor_tensor(below[:], logit[:], top[:].unsqueeze(1).to_broadcast(by_source), ALU.subtract)
            grown = soft.tile(by_source, F32, name="grown")
            nc.scalar.activation(grown[:], below[:], ACT.Exp)
            total = soft.tile([P, SPAN], F32, name="total")
            nc.vector.tensor_tensor(total[:], grown[:, 0, :], grown[:, 1, :], ALU.add)
            nc.vector.tensor_tensor(total[:], total[:], grown[:, 2, :], ALU.add)
            inverse = soft.tile([P, SPAN], F32, name="inverse")
            nc.vector.reciprocal(inverse[:], total[:])
            share = soft.tile(by_source, BF16, name="share")
            nc.vector.tensor_tensor(share[:], grown[:], inverse[:].unsqueeze(1).to_broadcast(by_source), ALU.mult)
            return share

        att = held.tile([P, len(SOURCES), N], BF16, name="att")

        parked = out[0 : QUARTER * len(SOURCES), N - BATCH : N].bitcast(BF16).rearrange("(r i) j -> r i j", i=len(SOURCES))

        def spread(t, share):
            for q in range(QUARTERS):
                first = t * BATCH + q * SPAN
                nc.sync.dma_start(parked[:, :, first : first + SPAN], share[q * QUARTER : (q + 1) * QUARTER, :, :])
            batch = slice(t * BATCH, (t + 1) * BATCH)
            for q in range(QUARTERS):
                nc.sync.dma_start(att[q * QUARTER : (q + 1) * QUARTER, :, batch], parked[:, :, batch])

        def weighted(i, p_i, first, width):
            whole = [P, MB, width]
            part = work.tile(whole, BF16, name="part%d" % i)
            nc.vector.tensor_tensor(part[:], p_i, att[:, i, first : first + width].unsqueeze(1).to_broadcast(whole), ALU.mult)
            return part

        both = held.tile([P, MB, N], BF16, name="both")
        out_blocks = out.rearrange("(a p) j -> p a j", p=P)

        def shorter_source(c):
            for a in range(MB):
                project(2, a, c * CHUNK, CHUNK, p2_sb[:, a, c * CHUNK : (c + 1) * CHUNK])

        def two_sources(c):
            here = slice(c * CHUNK, (c + 1) * CHUNK)
            part0 = weighted(0, p0_sb[:, :, here], c * CHUNK, CHUNK)
            part2 = weighted(2, p2_sb[:, :, here], c * CHUNK, CHUNK)
            nc.vector.tensor_tensor(both[:, :, here], part0[:], part2[:], ALU.add)

        def longer_source(t):
            first = t * BATCH
            for width in WIDTHS[t]:
                here = slice(first, first + width)
                for a in range(MB):
                    p1_sb = proj.tile([P, width], BF16, name="p1_sb")
                    project(1, a, first, width, p1_sb[:])
                    part1 = work.tile([P, width], BF16, name="part1")
                    nc.vector.tensor_tensor(part1[:], p1_sb[:], att[:, 1, here], ALU.mult)
                    mixed = done.tile([P, width], F32, name="mixed")
                    nc.vector.tensor_tensor(mixed[:], both[:, a, here], part1[:], ALU.add)
                    nc.sync.dma_start(out_blocks[:, a, here], mixed[:])
                first += width

        def last_piece():
            here = slice(N - LAST, N)
            deep = [P, depth[1], LAST]
            weighed = work.tile(deep, BF16, name="weighed")
            a_1 = att[:, 1, here]
            nc.vector.tensor_tensor(weighed[:], x_sb[1, 1][:, :, BATCH - LAST : BATCH], a_1.unsqueeze(1).to_broadcast(deep), ALU.mult)
            rest = work.tile([P, MB, LAST], F32, name="rest")
            for a in range(MB):
                nc.vector.scalar_tensor_tensor(rest[:, a, :], a_1, bias[1][:, a : a + 1], both[:, a, here], ALU.mult, ALU.add)
            for a in range(MB):
                acc = bank.tile([P, LAST], F32, name="acc")
                for k in range(depth[1]):
                    nc.tensor.matmul(
                        acc[:], w_sb[1][:, k, a * P : (a + 1) * P], weighed[:, k, :], start=(k == 0), stop=(k == depth[1] - 1)
                    )
                mixed = done.tile([P, LAST], F32, name="mixed")
                nc.vector.tensor_tensor(mixed[:], acc[:], rest[:, a, :], ALU.add)
                nc.sync.dma_start(out_blocks[:, a, here], mixed[:])

        shorter_source(1)
        c_all = constants(c_round)
        for t in range(N // BATCH):
            spread(t, weigh(t, c_all))
        two_sources(0)
        two_sources(1)
        longer_source(0)
        shorter_source(2)
        shorter_source(3)
        two_sources(2)
        two_sources(3)
        longer_source(1)
        last_piece()
